import numpy as np
import ml_dtypes


def mxq(x, axis, fmt="e4m3"):
    dtype, down = {"e4m3": (ml_dtypes.float8_e4m3fn, 7), "e5m2": (ml_dtypes.float8_e5m2, 14)}[fmt]
    v = np.moveaxis(np.asarray(x, np.float32).astype(ml_dtypes.bfloat16).astype(np.float64), axis, -1)
    blocks = v.reshape(v.shape[:-1] + (-1, 32))
    amax = np.abs(blocks).max(-1, keepdims=True)
    byte = np.maximum(np.where(amax > 0, np.frexp(amax)[1] - 1 + 127, 0) - down, 1)
    scale = np.exp2(byte - 127.0)
    codes = (blocks / scale).astype(np.float32).astype(dtype).astype(np.float64)
    return np.moveaxis((codes * scale).reshape(v.shape), -1, axis)


WIDE = False


def mx_kscale(k):
    if not WIDE:
        return np.ones(k)
    levels = np.array([10, -10, 5, -5, 0])
    a = np.random.permutation(np.resize(levels, k // 512 * 4)).reshape(k // 512, 4)
    idx = np.arange(k)
    return np.exp2(a[idx // 512, idx % 128 // 32])


BF16 = ml_dtypes.bfloat16


def bf(x):
    return np.asarray(x, np.float32).astype(BF16)


def f64(x):
    return np.asarray(x).astype(np.float64)


E2M1 = np.array([0.0, 0.5, 1.0, 1.5, 2.0, 3.0, 4.0, 6.0, -0.0, -0.5, -1.0, -1.5, -2.0, -3.0, -4.0, -6.0])


def pack_weight(w, fmt):
    k, n = w.shape
    w = f64(bf(w)).reshape(k // 32, 32, n)
    amax = np.abs(w).max(1)
    if fmt == "e4m3":
        byte = np.frexp(amax)[1] - 1 + 127 - 7
    else:
        mant, ex = np.frexp(amax / 6.0)
        byte = np.where(mant > 0.5, ex, ex - 1) + 127
    byte = np.clip(np.where(amax > 0, byte, 1), 1, 254)
    scaled = (w * np.exp2(127.0 - byte)[:, None, :]).reshape(k, n).astype(np.float32)
    by_word = np.ascontiguousarray(scaled.reshape(k // 512, 128, 4, n).transpose(0, 1, 3, 2))
    if fmt == "e4m3":
        words = by_word.astype(ml_dtypes.float8_e4m3fn).view(np.uint8)
    else:
        c = by_word.astype(ml_dtypes.float4_e2m1fn).view(np.uint8) & 0xF
        words = c[..., 0::2] | (c[..., 1::2] << 4)
    return np.ascontiguousarray(words), np.ascontiguousarray(byte.astype(np.uint8).reshape(k // 512, 16, n))


def unpack_weight(words, scales, fmt):
    g, p, n, _ = words.shape
    if fmt == "e4m3":
        vals = np.ascontiguousarray(words).view(ml_dtypes.float8_e4m3fn).astype(np.float64)
    else:
        nib = np.empty((g, p, n, 4), np.uint8)
        nib[..., 0::2] = words & 0xF
        nib[..., 1::2] = words >> 4
        vals = E2M1[nib]
    vals = vals * np.repeat(np.exp2(scales.astype(np.float64) - 127.0), 8, axis=1)[..., None]
    return vals.transpose(0, 1, 3, 2).reshape(g * 512, n)

def pack4(w):
    words, scales = pack_weight(w, "e2m1")
    return words.reshape(words.shape[0], 128, -1), scales


def unpack4(words, scales):
    return unpack_weight(words.reshape(words.shape[0], 128, -1, 2), scales, "e2m1")


B, EN_MID, DE_MID = 1024, 2048, 4096
K1 = EN_MID // 2
K2 = DE_MID // 2


def setup_inputs():
    s = mx_kscale(K1)
    in_data = np.random.standard_normal((B, K1, 2)) * s[None, :, None]
    w = np.random.standard_normal((DE_MID, K1)) / np.sqrt(K1) / s[None, :]
    W_words, W_scales = pack4(w.T)
    return {"in_data": bf(in_data.reshape(B, EN_MID)),
            "W_words": W_words,
            "W_scales": W_scales,
            "bias": bf(np.random.standard_normal(DE_MID) * 0.25)}


def reference(in_data, W_words, W_scales, bias):
    Bsz = in_data.shape[0]
    x_imag = f64(in_data).reshape(Bsz, K1, 2)[:, :, 1]
    tmp = mxq(x_imag, 1, "e4m3") @ unpack4(W_words, W_scales)
    act = np.maximum(tmp + f64(bias), 0.0)
    out_r = act[:, :K2] - act[:, K2:]
    out = np.stack([out_r, np.zeros_like(out_r)], axis=2)
    return out.reshape(Bsz, DE_MID, 1)

@@ -1,0 +1,165 @@
+from contextlib import ExitStack
+
+import concourse.mybir as mybir
+from concourse.masks import make_identity
+
+F32 = mybir.dt.float32
+BF16 = mybir.dt.bfloat16
+I32 = mybir.dt.int32
+U32 = mybir.dt.uint32
+U8 = mybir.dt.uint8
+FP8X4 = mybir.dt.float8_e4m3fn_x4
+FP4X4 = mybir.dt.float4_e2m1fn_x4
+ALU = mybir.AluOpType
+
+P = 128
+B = 1024
+K = 1024
+N = 4096
+HALF = N // 2
+G = K // 512
+NB = B // P
+JC = 512
+NJ = HALF // JC
+NRZ = 4
+
+FLOPS = 2 * B * K * N
+
+
+def tile_middlelayer_kernel(tc, in_data, W_words, W_scales, bias, out):
+    nc = tc.nc
+    out2 = out.rearrange("b n o -> b (n o)")
+    with ExitStack() as ctx:
+        const = ctx.enter_context(tc.tile_pool(name="const", bufs=1))
+        xin_pool = ctx.enter_context(tc.tile_pool(name="xin", bufs=NB))
+        xprep = ctx.enter_context(tc.tile_pool(name="xprep", bufs=3))
+        work = ctx.enter_context(tc.tile_pool(name="work", bufs=4))
+        outp = ctx.enter_context(tc.tile_pool(name="outp", bufs=6))
+        mxps = ctx.enter_context(tc.psum_pool(name="mxps", bufs=6))
+        tpps = ctx.enter_context(tc.psum_pool(name="tpps", bufs=2))
+
+        ws = const.tile([P, G, N], U8, align_bytes=64)
+        wq = const.tile([P, G, 2 * N], U8, align_bytes=64)
+        xq = const.tile([P, NB, G, P], U32, align_bytes=64)
+        xs = const.tile([P, NB, G, P], U8, align_bytes=64)
+        biasrow = const.tile([P, N], BF16)
+        bias_bc = const.tile([P, N], BF16)
+        ones = const.tile([P, P], BF16)
+        ident = const.tile([P, P], F32)
+        rzs = [const.tile([P, 2, JC], F32, name="rz%d" % i) for i in range(NRZ)]
+
+        nc.vector.memset(ws[:].bitcast(I32), 0)
+        nc.vector.memset(biasrow[:].bitcast(I32), 0)
+        make_identity(nc, ident[:])
+        nc.gpsimd.memset(ones[:], 1.0)
+        for rz in rzs:
+            nc.gpsimd.memset(rz[:, 1, :], 0.0)
+
+        xins = []
+
+        def load_x(bt):
+            xin = xin_pool.tile([P, 2 * K], BF16)
+            nc.sync.dma_start(out=xin[:], in_=in_data[P * bt : P * (bt + 1), :])
+            xins.append(xin)
+
+        def load_w(jc):
+            for half in range(2):
+                for g in range(G):
+                    a = 2 * (HALF * half + JC * jc)
+                    nc.sync.dma_start(
+                        out=wq[:, g, a : a + 2 * JC].bitcast(I32),
+                        in_=W_words[g, :, a : a + 2 * JC].bitcast(I32),
+                    )
+
+        load_x(0)
+        for g in range(G):
+            for b2 in range(2):
+                for r in range(4):
+                    nc.sync.dma_start(
+                        out=ws[32 * b2 + r : P : 64, g, :].bitcast(I32),
+                        in_=W_scales[g, 4 * b2 + r : 16 : 8, :].bitcast(I32),
+                    )
+        nc.scalar.dma_start(out=biasrow[0:1, :], in_=bias.rearrange("(o n) -> o n", o=1))
+        load_w(0)
+        load_w(1)
+        load_x(1)
+        load_w(2)
+        load_w(3)
+        for bt in range(2, NB):
+            load_x(bt)
+
+        def prep(bt):
+            xin = xins[bt]
+            xc = xprep.tile([P, K], BF16)
+            imag = xin[:, 1 : 2 * K : 2].rearrange("b (g p u e) -> b g u p e", g=G, p=P, u=2, e=2)
+            dst = xc[:].rearrange("b (g u p e) -> b g u p e", g=G, u=2, p=P, e=2)
+            for g in range(G):
+                if bt < 2:
+                    nc.vector.tensor_copy(out=dst[:, g], in_=imag[:, g])
+                else:
+                    nc.gpsimd.tensor_scalar(
+                        out=dst[:, g], in0=imag[:, g], scalar1=1.0, scalar2=0.0, op0=ALU.mult, op1=ALU.add
+                    )
+            words = xc[:].bitcast(F32)
+            tp = tpps.tile([P, 2 * G, P], F32)
+            for gu in range(2 * G):
+                nc.tensor.transpose(tp[:, gu, :], words[:, P * gu : P * (gu + 1)], ident[:])
+            grp = xprep.tile([P, 4 * G * P], BF16, align_bytes=64)
+            nc.scalar.copy(
+                out=grp[:].bitcast(F32).rearrange("p (g b u) -> p g b u", g=G, b=P, u=2),
+                in_=tp[:].rearrange("p (g u) b -> p g b u", g=G, u=2),
+            )
+            nc.vector.quantize_mx(
+                out=xq[:, bt].rearrange("p g b -> p (g b)").bitcast(FP8X4),
+                scales=xs[:, bt].rearrange("p g b -> p (g b)"),
+                in_=grp[:],
+            )
+
+        def spread_bias():
+            for i, c in enumerate((0, 4, 1, 5, 2, 6, 3, 7)):
+                ps = mxps.tile([P, JC], F32, tag="mx")
+                nc.tensor.matmul(out=ps[:], lhsT=ones[:], rhs=biasrow[:, JC * c : JC * (c + 1)], start=True, stop=True)
+                if i % 2 == 0:
+                    nc.vector.tensor_copy(out=bias_bc[:, JC * c : JC * (c + 1)], in_=ps[:])
+                else:
+                    nc.scalar.copy(out=bias_bc[:, JC * c : JC * (c + 1)], in_=ps[:])
+
+        def unit(bt, jc):
+            sums = []
+            for half in range(2):
+                n0 = HALF * half + JC * jc
+                ps = mxps.tile([P, JC], F32, tag="mx")
+                for g in range(G):
+                    nc.tensor.matmul_mx(
+                        out=ps[:],
+                        lhsT=xq[:, bt, g, :].bitcast(FP8X4),
+                        lhsT_scale=xs[:, bt, g, :],
+                        rhs=wq[:, g, 2 * n0 : 2 * (n0 + JC)].bitcast(FP4X4),
+                        rhs_scale=ws[:, g, n0 : n0 + JC],
+                        start=(g == 0),
+                        stop=(g == G - 1),
+                    )
+                sums.append(ps)
+            n2 = work.tile([P, JC], F32)
+            nc.vector.tensor_tensor(
+                out=n2[:], in0=sums[1][:], in1=bias_bc[:, HALF + JC * jc : HALF + JC * (jc + 1)], op=ALU.add
+            )
+            n1 = work.tile([P, JC], F32)
+            nc.vector.tensor_tensor(out=n1[:], in0=sums[0][:], in1=bias_bc[:, JC * jc : JC * (jc + 1)], op=ALU.add)
+            q2 = work.tile([P, JC], F32)
+            nc.gpsimd.tensor_scalar(out=q2[:], in0=n2[:], scalar1=0.0, scalar2=0.0, op0=ALU.max, op1=ALU.add)
+            rz = rzs[(NJ * bt + jc) % NRZ]
+            nc.vector.scalar_tensor_tensor(
+                out=rz[:, 0, :], in0=n1[:], scalar=0.0, in1=q2[:], op0=ALU.max, op1=ALU.subtract
+            )
+            ot = outp.tile([P, 2 * JC], F32)
+            nc.scalar.copy(out=ot[:].rearrange("p (j e) -> p j e", e=2), in_=rz[:].rearrange("p e j -> p j e"))
+            nc.scalar.dma_start(out=out2[P * bt : P * (bt + 1), 2 * JC * jc : 2 * JC * (jc + 1)], in_=ot[:])
+
+        prep(0)
+        spread_bias()
+        for bt in range(NB):
+            if bt + 1 < NB:
+                prep(bt + 1)
+            for jc in range(NJ):
+                unit(bt, jc)

@@ -11,6 +11,7 @@ U8 = mybir.dt.uint8
 FP8X4 = mybir.dt.float8_e4m3fn_x4
 FP4X4 = mybir.dt.float4_e2m1fn_x4
 ALU = mybir.AluOpType
+ACT = mybir.ActivationFunctionType
 
 P = 128
 B = 1024
@@ -37,6 +38,7 @@ def tile_middlelayer_kernel(tc, in_data, W_words, W_scales, bias, out):
         outp = ctx.enter_context(tc.tile_pool(name="outp", bufs=6))
         mxps = ctx.enter_context(tc.psum_pool(name="mxps", bufs=6))
         tpps = ctx.enter_context(tc.psum_pool(name="tpps", bufs=2))
+        ctx.enter_context(tc.manual_schedule())
 
         ws = const.tile([P, G, N], U8, align_bytes=64)
         wq = const.tile([P, G, 2 * N], U8, align_bytes=64)
@@ -115,16 +117,15 @@ def tile_middlelayer_kernel(tc, in_data, W_words, W_scales, bias, out):
                 in_=grp[:],
             )
 
-        def spread_bias():
-            for i, c in enumerate((0, 4, 1, 5, 2, 6, 3, 7)):
-                ps = mxps.tile([P, JC], F32, tag="mx")
-                nc.tensor.matmul(out=ps[:], lhsT=ones[:], rhs=biasrow[:, JC * c : JC * (c + 1)], start=True, stop=True)
-                if i % 2 == 0:
-                    nc.vector.tensor_copy(out=bias_bc[:, JC * c : JC * (c + 1)], in_=ps[:])
-                else:
-                    nc.scalar.copy(out=bias_bc[:, JC * c : JC * (c + 1)], in_=ps[:])
+        def spread_bias(c, eng):
+            ps = mxps.tile([P, JC], F32, tag="mx")
+            nc.tensor.matmul(out=ps[:], lhsT=ones[:], rhs=biasrow[:, JC * c : JC * (c + 1)], start=True, stop=True)
+            if eng == 0:
+                nc.vector.tensor_copy(out=bias_bc[:, JC * c : JC * (c + 1)], in_=ps[:])
+            else:
+                nc.scalar.copy(out=bias_bc[:, JC * c : JC * (c + 1)], in_=ps[:])
 
-        def unit(bt, jc):
+        def front(bt, jc):
             sums = []
             for half in range(2):
                 n0 = HALF * half + JC * jc
@@ -147,19 +148,37 @@ def tile_middlelayer_kernel(tc, in_data, W_words, W_scales, bias, out):
             n1 = work.tile([P, JC], F32)
             nc.vector.tensor_tensor(out=n1[:], in0=sums[0][:], in1=bias_bc[:, JC * jc : JC * (jc + 1)], op=ALU.add)
             q2 = work.tile([P, JC], F32)
-            nc.gpsimd.tensor_scalar(out=q2[:], in0=n2[:], scalar1=0.0, scalar2=0.0, op0=ALU.max, op1=ALU.add)
-            rz = rzs[(NJ * bt + jc) % NRZ]
+            nc.scalar.activation(out=q2[:], in_=n2[:], func=ACT.Relu)
+            return n1, q2
+
+        def back(bt, jc, n1, q2):
+            u = NJ * bt + jc
+            rz = rzs[u % NRZ]
             nc.vector.scalar_tensor_tensor(
                 out=rz[:, 0, :], in0=n1[:], scalar=0.0, in1=q2[:], op0=ALU.max, op1=ALU.subtract
             )
             ot = outp.tile([P, 2 * JC], F32)
-            nc.scalar.copy(out=ot[:].rearrange("p (j e) -> p j e", e=2), in_=rz[:].rearrange("p e j -> p j e"))
-            nc.scalar.dma_start(out=out2[P * bt : P * (bt + 1), 2 * JC * jc : 2 * JC * (jc + 1)], in_=ot[:])
+            pairs = ot[:].rearrange("p (j e) -> p j e", e=2)
+            planes = rz[:].rearrange("p e j -> p j e")
+            if u % 2 == 0:
+                nc.scalar.copy(out=pairs, in_=planes)
+            else:
+                nc.gpsimd.tensor_scalar(out=pairs, in0=planes, scalar1=1.0, scalar2=0.0, op0=ALU.mult, op1=ALU.add)
+            nc.sync.dma_start(out=out2[P * bt : P * (bt + 1), 2 * JC * jc : 2 * JC * (jc + 1)], in_=ot[:])
 
         prep(0)
-        spread_bias()
+        spread_bias(4, 0)
+        spread_bias(0, 0)
+        pending = None
         for bt in range(NB):
-            if bt + 1 < NB:
-                prep(bt + 1)
             for jc in range(NJ):
-                unit(bt, jc)
+                cur = (bt, jc) + front(bt, jc)
+                if bt == 0 and jc + 1 < NJ:
+                    spread_bias(4 + jc + 1, 1)
+                    spread_bias(jc + 1, 1)
+                if jc == 0 and bt + 1 < NB:
+                    prep(bt + 1)
+                if pending is not None:
+                    back(*pending)
+                pending = cur
+        back(*pending)

@@ -38,7 +38,6 @@ def tile_middlelayer_kernel(tc, in_data, W_words, W_scales, bias, out):
         outp = ctx.enter_context(tc.tile_pool(name="outp", bufs=6))
         mxps = ctx.enter_context(tc.psum_pool(name="mxps", bufs=6))
         tpps = ctx.enter_context(tc.psum_pool(name="tpps", bufs=2))
-        ctx.enter_context(tc.manual_schedule())
 
         ws = const.tile([P, G, N], U8, align_bytes=64)
         wq = const.tile([P, G, 2 * N], U8, align_bytes=64)

@@ -22,7 +22,10 @@ G = K // 512
 NB = B // P
 JC = 512
 NJ = HALF // JC
-NRZ = 4
+NRZ = 6
+SORT = ("v", "s", "g", "s", "g", "g", "g", "g")
+IL = ("s", "g", "s", "g", "s", "g", "s", "g", "s", "g", "s", "g", "s", "g", "s", "g", "s", "g", "s", "g", "s", "g", "s", "g", "v", "g", "v", "g", "s", "g", "v", "s")
+PLAN = (((3, 0), (3, 1), (3, 2)), ((3, 3), (4, 0), (5, 0)), ((6, 0), (7, 0), (4, 1)), ((5, 1), (6, 1), (7, 1)), ((4, 2), (5, 2)), ((6, 2), (7, 2), (4, 3)), ((5, 3), (6, 3), (7, 3)), ())
 
 FLOPS = 2 * B * K * N
 
@@ -33,44 +36,51 @@ def tile_middlelayer_kernel(tc, in_data, W_words, W_scales, bias, out):
     with ExitStack() as ctx:
         const = ctx.enter_context(tc.tile_pool(name="const", bufs=1))
         xin_pool = ctx.enter_context(tc.tile_pool(name="xin", bufs=NB))
-        xprep = ctx.enter_context(tc.tile_pool(name="xprep", bufs=3))
-        work = ctx.enter_context(tc.tile_pool(name="work", bufs=4))
-        outp = ctx.enter_context(tc.tile_pool(name="outp", bufs=6))
-        mxps = ctx.enter_context(tc.psum_pool(name="mxps", bufs=6))
-        tpps = ctx.enter_context(tc.psum_pool(name="tpps", bufs=2))
+        xc_pool = ctx.enter_context(tc.tile_pool(name="xc", bufs=4))
+        grp_pool = ctx.enter_context(tc.tile_pool(name="grp", bufs=3))
+        n1_pool = ctx.enter_context(tc.tile_pool(name="n1p", bufs=24))
+        rbt_pool = ctx.enter_context(tc.tile_pool(name="rbtp", bufs=8))
+        outp = ctx.enter_context(tc.tile_pool(name="outp", bufs=8))
+        mxps = ctx.enter_context(tc.psum_pool(name="mxps", bufs=4))
+        tbps = ctx.enter_context(tc.psum_pool(name="tbps", bufs=4))
+        ctx.enter_context(tc.manual_schedule())
 
         ws = const.tile([P, G, N], U8, align_bytes=64)
         wq = const.tile([P, G, 2 * N], U8, align_bytes=64)
-        xq = const.tile([P, NB, G, P], U32, align_bytes=64)
-        xs = const.tile([P, NB, G, P], U8, align_bytes=64)
-        biasrow = const.tile([P, N], BF16)
-        bias_bc = const.tile([P, N], BF16)
+        xq = const.tile([P, G, B], U32, align_bytes=64)
+        xs = const.tile([P, G, B], U8, align_bytes=64)
+        biasrow = const.tile([P, HALF], BF16)
+        bias_bc = const.tile([P, HALF], BF16)
+        brows = const.tile([P, P], BF16)
+        bias_t = const.tile([P, N // P], F32)
         ones = const.tile([P, P], BF16)
         ident = const.tile([P, P], F32)
+        identb = const.tile([P, P], BF16)
         rzs = [const.tile([P, 2, JC], F32, name="rz%d" % i) for i in range(NRZ)]
 
         nc.vector.memset(ws[:].bitcast(I32), 0)
         nc.vector.memset(biasrow[:].bitcast(I32), 0)
+        nc.vector.memset(brows[:].bitcast(I32), 0)
         make_identity(nc, ident[:])
+        make_identity(nc, identb[:])
         nc.gpsimd.memset(ones[:], 1.0)
         for rz in rzs:
             nc.gpsimd.memset(rz[:, 1, :], 0.0)
 
-        xins = []
+        xins = {}
 
         def load_x(bt):
             xin = xin_pool.tile([P, 2 * K], BF16)
             nc.sync.dma_start(out=xin[:], in_=in_data[P * bt : P * (bt + 1), :])
-            xins.append(xin)
+            xins[bt] = xin
 
-        def load_w(jc):
-            for half in range(2):
-                for g in range(G):
-                    a = 2 * (HALF * half + JC * jc)
-                    nc.sync.dma_start(
-                        out=wq[:, g, a : a + 2 * JC].bitcast(I32),
-                        in_=W_words[g, :, a : a + 2 * JC].bitcast(I32),
-                    )
+        def load_w(half):
+            for g in range(G):
+                a = 2 * HALF * half
+                nc.sync.dma_start(
+                    out=wq[:, g, a : a + 2 * HALF].bitcast(I32),
+                    in_=W_words[g, :, a : a + 2 * HALF].bitcast(I32),
+                )
 
         load_x(0)
         for g in range(G):
@@ -80,104 +90,168 @@ def tile_middlelayer_kernel(tc, in_data, W_words, W_scales, bias, out):
                         out=ws[32 * b2 + r : P : 64, g, :].bitcast(I32),
                         in_=W_scales[g, 4 * b2 + r : 16 : 8, :].bitcast(I32),
                     )
-        nc.scalar.dma_start(out=biasrow[0:1, :], in_=bias.rearrange("(o n) -> o n", o=1))
+        nc.scalar.dma_start(out=biasrow[0:1, :], in_=bias[0:HALF].rearrange("(o n) -> o n", o=1))
+        nc.scalar.dma_start(out=brows[0 : N // P, :], in_=bias.rearrange("(t p) -> t p", p=P))
         load_w(0)
+        for bt in range(1, 4):
+            load_x(bt)
         load_w(1)
-        load_x(1)
-        load_w(2)
-        load_w(3)
-        for bt in range(2, NB):
+        for bt in range(4, NB):
             load_x(bt)
 
-        def prep(bt):
-            xin = xins[bt]
-            xc = xprep.tile([P, K], BF16)
-            imag = xin[:, 1 : 2 * K : 2].rearrange("b (g p u e) -> b g u p e", g=G, p=P, u=2, e=2)
+        xcs = {}
+        tps = {}
+        grps = {}
+
+        def sort(bt):
+            xc = xc_pool.tile([P, K], BF16)
+            imag = xins[bt][:, 1 : 2 * K : 2].rearrange("b (g p u e) -> b g u p e", g=G, p=P, u=2, e=2)
             dst = xc[:].rearrange("b (g u p e) -> b g u p e", g=G, u=2, p=P, e=2)
             for g in range(G):
-                if bt < 2:
+                if SORT[bt] == "v":
                     nc.vector.tensor_copy(out=dst[:, g], in_=imag[:, g])
+                elif SORT[bt] == "s":
+                    nc.scalar.copy(out=dst[:, g], in_=imag[:, g])
                 else:
                     nc.gpsimd.tensor_scalar(
                         out=dst[:, g], in0=imag[:, g], scalar1=1.0, scalar2=0.0, op0=ALU.mult, op1=ALU.add
                     )
-            words = xc[:].bitcast(F32)
-            tp = tpps.tile([P, 2 * G, P], F32)
+            xcs[bt] = xc
+
+        def turn(bt):
+            words = xcs[bt][:].bitcast(F32)
+            tp = mxps.tile([P, 2 * G, P], F32, tag="mx")
             for gu in range(2 * G):
                 nc.tensor.transpose(tp[:, gu, :], words[:, P * gu : P * (gu + 1)], ident[:])
-            grp = xprep.tile([P, 4 * G * P], BF16, align_bytes=64)
+            grp = grp_pool.tile([P, 4 * G * P], BF16, align_bytes=64)
             nc.scalar.copy(
                 out=grp[:].bitcast(F32).rearrange("p (g b u) -> p g b u", g=G, b=P, u=2),
                 in_=tp[:].rearrange("p (g u) b -> p g b u", g=G, u=2),
             )
-            nc.vector.quantize_mx(
-                out=xq[:, bt].rearrange("p g b -> p (g b)").bitcast(FP8X4),
-                scales=xs[:, bt].rearrange("p g b -> p (g b)"),
-                in_=grp[:],
-            )
+            grps[bt] = grp
+
+        def quant(bt):
+            for g in range(G):
+                nc.vector.quantize_mx(
+                    out=xq[:, g, P * bt : P * (bt + 1)].bitcast(FP8X4),
+                    scales=xs[:, g, P * bt : P * (bt + 1)],
+                    in_=grps[bt][:, 4 * P * g : 4 * P * (g + 1)],
+                )
 
         def spread_bias(c, eng):
             ps = mxps.tile([P, JC], F32, tag="mx")
             nc.tensor.matmul(out=ps[:], lhsT=ones[:], rhs=biasrow[:, JC * c : JC * (c + 1)], start=True, stop=True)
-            if eng == 0:
+            if eng == "v":
                 nc.vector.tensor_copy(out=bias_bc[:, JC * c : JC * (c + 1)], in_=ps[:])
             else:
                 nc.scalar.copy(out=bias_bc[:, JC * c : JC * (c + 1)], in_=ps[:])
 
-        def front(bt, jc):
-            sums = []
-            for half in range(2):
-                n0 = HALF * half + JC * jc
-                ps = mxps.tile([P, JC], F32, tag="mx")
-                for g in range(G):
-                    nc.tensor.matmul_mx(
-                        out=ps[:],
-                        lhsT=xq[:, bt, g, :].bitcast(FP8X4),
-                        lhsT_scale=xs[:, bt, g, :],
-                        rhs=wq[:, g, 2 * n0 : 2 * (n0 + JC)].bitcast(FP4X4),
-                        rhs_scale=ws[:, g, n0 : n0 + JC],
-                        start=(g == 0),
-                        stop=(g == G - 1),
-                    )
-                sums.append(ps)
-            n2 = work.tile([P, JC], F32)
-            nc.vector.tensor_tensor(
-                out=n2[:], in0=sums[1][:], in1=bias_bc[:, HALF + JC * jc : HALF + JC * (jc + 1)], op=ALU.add
-            )
-            n1 = work.tile([P, JC], F32)
-            nc.vector.tensor_tensor(out=n1[:], in0=sums[0][:], in1=bias_bc[:, JC * jc : JC * (jc + 1)], op=ALU.add)
-            q2 = work.tile([P, JC], F32)
-            nc.scalar.activation(out=q2[:], in_=n2[:], func=ACT.Relu)
-            return n1, q2
+        n1s = {}
 
-        def back(bt, jc, n1, q2):
-            u = NJ * bt + jc
+        def first_half(bt, jc):
+            n0 = JC * jc
+            ps = mxps.tile([P, JC], F32, tag="mx")
+            for g in range(G):
+                nc.tensor.matmul_mx(
+                    out=ps[:],
+                    lhsT=xq[:, g, P * bt : P * (bt + 1)].bitcast(FP8X4),
+                    lhsT_scale=xs[:, g, P * bt : P * (bt + 1)],
+                    rhs=wq[:, g, 2 * n0 : 2 * (n0 + JC)].bitcast(FP4X4),
+                    rhs_scale=ws[:, g, n0 : n0 + JC],
+                    start=(g == 0),
+                    stop=(g == G - 1),
+                )
+            n1 = n1_pool.tile([P, JC], F32)
+            nc.vector.tensor_tensor(out=n1[:], in0=ps[:], in1=bias_bc[:, n0 : n0 + JC], op=ALU.add)
+            n1s[(bt, jc)] = n1
+
+        def second_half(h, jc, jt):
+            n0 = HALF + JC * jc + P * jt
+            ps = mxps.tile([P, JC], F32, tag="mx")
+            for g in range(G):
+                nc.tensor.matmul_mx(
+                    out=ps[:],
+                    lhsT=wq[:, g, 2 * n0 : 2 * (n0 + P)].bitcast(FP4X4),
+                    lhsT_scale=ws[:, g, n0 : n0 + P],
+                    rhs=xq[:, g, JC * h : JC * (h + 1)].bitcast(FP8X4),
+                    rhs_scale=xs[:, g, JC * h : JC * (h + 1)],
+                    start=(g == 0),
+                    stop=(g == G - 1),
+                )
+            rbt = rbt_pool.tile([P, JC], F32)
+            nc.scalar.activation(out=rbt[:], in_=ps[:], func=ACT.Relu, bias=bias_t[:, n0 // P : n0 // P + 1], scale=1.0)
+            return rbt
+
+        def turn_back(rbts, i):
+            tb = tbps.tile([P, JC], F32)
+            for jt in range(4):
+                nc.tensor.transpose(tb[:, P * jt : P * (jt + 1)], rbts[jt][:, P * i : P * (i + 1)], ident[:])
+            return tb
+
+        counter = [0]
+
+        def finish(bt, jc, tb):
+            u = counter[0]
+            counter[0] = u + 1
             rz = rzs[u % NRZ]
             nc.vector.scalar_tensor_tensor(
-                out=rz[:, 0, :], in0=n1[:], scalar=0.0, in1=q2[:], op0=ALU.max, op1=ALU.subtract
+                out=rz[:, 0, :], in0=n1s[(bt, jc)][:], scalar=0.0, in1=tb[:], op0=ALU.max, op1=ALU.subtract
             )
             ot = outp.tile([P, 2 * JC], F32)
             pairs = ot[:].rearrange("p (j e) -> p j e", e=2)
             planes = rz[:].rearrange("p e j -> p j e")
-            if u % 2 == 0:
+            if IL[u] == "s":
                 nc.scalar.copy(out=pairs, in_=planes)
-            else:
+            elif IL[u] == "g":
                 nc.gpsimd.tensor_scalar(out=pairs, in0=planes, scalar1=1.0, scalar2=0.0, op0=ALU.mult, op1=ALU.add)
+            else:
+                nc.vector.tensor_copy(out=pairs, in_=planes)
             nc.sync.dma_start(out=out2[P * bt : P * (bt + 1), 2 * JC * jc : 2 * JC * (jc + 1)], in_=ot[:])
 
-        prep(0)
-        spread_bias(4, 0)
-        spread_bias(0, 0)
-        pending = None
-        for bt in range(NB):
-            for jc in range(NJ):
-                cur = (bt, jc) + front(bt, jc)
-                if bt == 0 and jc + 1 < NJ:
-                    spread_bias(4 + jc + 1, 1)
-                    spread_bias(jc + 1, 1)
-                if jc == 0 and bt + 1 < NB:
-                    prep(bt + 1)
-                if pending is not None:
-                    back(*pending)
-                pending = cur
-        back(*pending)
+        sort(0)
+        turn(0)
+        quant(0)
+        spread_bias(0, "v")
+        for c in range(1, NJ):
+            spread_bias(c, "s")
+        pst = mxps.tile([P, P], F32, tag="mx")
+        nc.tensor.matmul(out=pst[:], lhsT=brows[:], rhs=identb[:], start=True, stop=True)
+        nc.vector.tensor_copy(out=bias_t[:], in_=pst[:, 0 : N // P])
+        sort(2)
+        for jc in range(NJ):
+            first_half(0, jc)
+        sort(1)
+        turn(1)
+        quant(1)
+        sort(3)
+        first_half(1, 0)
+        turn(2)
+        quant(2)
+        first_half(1, 1)
+        turn(3)
+        quant(3)
+        first_half(1, 2)
+        first_half(1, 3)
+        for jc in range(NJ):
+            first_half(2, jc)
+        groups = {}
+        for q in range(9):
+            h, jc = q // NJ, q % NJ
+            if q == 0:
+                for bt in range(4, NB):
+                    sort(bt)
+            if q < 8:
+                rbts = [second_half(h, jc, jt) for jt in range(4)]
+            if q >= 1:
+                ph, pjc, tbs = groups[q - 1]
+                for i in range(4):
+                    finish(4 * ph + i, pjc, tbs[i])
+            if q < 8:
+                for bt, j in PLAN[q]:
+                    first_half(bt, j)
+                groups[q] = (h, jc, [turn_back(rbts, i) for i in range(4)])
+            if q < 2:
+                turn(4 + 2 * q)
+                turn(5 + 2 * q)
+                quant(4 + 2 * q)
+                quant(5 + 2 * q)

@@ -24,8 +24,8 @@ JC = 512
 NJ = HALF // JC
 NRZ = 6
 SORT = ("v", "s", "g", "s", "g", "g", "g", "g")
-IL = ("s", "g", "s", "g", "s", "g", "s", "g", "s", "g", "s", "g", "s", "g", "s", "g", "s", "g", "s", "g", "s", "g", "s", "g", "v", "g", "v", "g", "s", "g", "v", "s")
-PLAN = (((3, 0), (3, 1), (3, 2)), ((3, 3), (4, 0), (5, 0)), ((6, 0), (7, 0), (4, 1)), ((5, 1), (6, 1), (7, 1)), ((4, 2), (5, 2)), ((6, 2), (7, 2), (4, 3)), ((5, 3), (6, 3), (7, 3)), ())
+IL = ("g", "s", "g", "g", "g", "s", "g", "g", "s", "g", "g", "s", "s", "s", "g", "s", "g", "g", "g", "v", "g", "s", "g", "g", "g", "g", "s", "g", "s", "g", "s", "g")
+PLAN = (((2, 1), (3, 1), (1, 2)), ((2, 2), (3, 2), (1, 3)), ((2, 3), (3, 3), (4, 0)), ((5, 0), (6, 0), (7, 0)), ((4, 1), (5, 1), (6, 1)), ((7, 1), (4, 2), (5, 2)), ((6, 2), (7, 2), (4, 3)), ((5, 3), (6, 3), (7, 3)))
 
 FLOPS = 2 * B * K * N
 
@@ -230,10 +230,8 @@ def tile_middlelayer_kernel(tc, in_data, W_words, W_scales, bias, out):
         first_half(1, 1)
         turn(3)
         quant(3)
-        first_half(1, 2)
-        first_half(1, 3)
-        for jc in range(NJ):
-            first_half(2, jc)
+        first_half(2, 0)
+        first_half(3, 0)
         groups = {}
         for q in range(9):
             h, jc = q // NJ, q % NJ

@@ -14,242 +14,260 @@ ALU = mybir.AluOpType
 ACT = mybir.ActivationFunctionType
 
 P = 128
-B = 1024
+ROWS = 1024
 K = 1024
-N = 4096
-HALF = N // 2
-G = K // 512
-NB = B // P
-JC = 512
-NJ = HALF // JC
-NRZ = 6
-SORT = ("v", "s", "g", "s", "g", "g", "g", "g")
-IL = ("g", "s", "g", "g", "g", "s", "g", "g", "s", "g", "g", "s", "s", "s", "g", "s", "g", "g", "g", "v", "g", "s", "g", "g", "g", "g", "s", "g", "s", "g", "s", "g")
-PLAN = (((2, 1), (3, 1), (1, 2)), ((2, 2), (3, 2), (1, 3)), ((2, 3), (3, 3), (4, 0)), ((5, 0), (6, 0), (7, 0)), ((4, 1), (5, 1), (6, 1)), ((7, 1), (4, 2), (5, 2)), ((6, 2), (7, 2), (4, 3)), ((5, 3), (6, 3), (7, 3)))
+COLS = 4096
+HALF = COLS // 2
+PASSES = K // 512
+ROW_TILES = ROWS // P
+CHUNK = 512
+CHUNKS = HALF // CHUNK
+TILES_MOVING = CHUNK // P
+ROUNDS = (ROW_TILES // TILES_MOVING) * CHUNKS
+LEAD = ((0, 0), (0, 1), (0, 2), (0, 3), (1, 0), (1, 1), (2, 0), (3, 0))
+UNITS_A_ROUND = (ROW_TILES * CHUNKS - len(LEAD)) // ROUNDS
+ZERO_PLANE_TILES = 6
 
-FLOPS = 2 * B * K * N
+FLOPS = 2 * ROWS * K * COLS
 
 
 def tile_middlelayer_kernel(tc, in_data, W_words, W_scales, bias, out):
     nc = tc.nc
-    out2 = out.rearrange("b n o -> b (n o)")
+    out_rows = out.rearrange("b n o -> b (n o)")
     with ExitStack() as ctx:
         const = ctx.enter_context(tc.tile_pool(name="const", bufs=1))
-        xin_pool = ctx.enter_context(tc.tile_pool(name="xin", bufs=NB))
-        xc_pool = ctx.enter_context(tc.tile_pool(name="xc", bufs=4))
-        grp_pool = ctx.enter_context(tc.tile_pool(name="grp", bufs=3))
-        n1_pool = ctx.enter_context(tc.tile_pool(name="n1p", bufs=24))
-        rbt_pool = ctx.enter_context(tc.tile_pool(name="rbtp", bufs=8))
-        outp = ctx.enter_context(tc.tile_pool(name="outp", bufs=8))
-        mxps = ctx.enter_context(tc.psum_pool(name="mxps", bufs=4))
-        tbps = ctx.enter_context(tc.psum_pool(name="tbps", bufs=4))
+        xin_pool = ctx.enter_context(tc.tile_pool(name="xin", bufs=ROW_TILES))
+        sorted_pool = ctx.enter_context(tc.tile_pool(name="sorted", bufs=4))
+        grouped_pool = ctx.enter_context(tc.tile_pool(name="grouped", bufs=3))
+        first_pool = ctx.enter_context(tc.tile_pool(name="first", bufs=24))
+        second_pool = ctx.enter_context(tc.tile_pool(name="second", bufs=2 * TILES_MOVING))
+        store_pool = ctx.enter_context(tc.tile_pool(name="store", bufs=8))
+        sums_pool = ctx.enter_context(tc.psum_pool(name="sums", bufs=4))
+        back_pool = ctx.enter_context(tc.psum_pool(name="back", bufs=TILES_MOVING))
         ctx.enter_context(tc.manual_schedule())
 
-        ws = const.tile([P, G, N], U8, align_bytes=64)
-        wq = const.tile([P, G, 2 * N], U8, align_bytes=64)
-        xq = const.tile([P, G, B], U32, align_bytes=64)
-        xs = const.tile([P, G, B], U8, align_bytes=64)
-        biasrow = const.tile([P, HALF], BF16)
-        bias_bc = const.tile([P, HALF], BF16)
-        brows = const.tile([P, P], BF16)
-        bias_t = const.tile([P, N // P], F32)
+        w_scales = const.tile([P, PASSES, COLS], U8, align_bytes=64)
+        w_words = const.tile([P, PASSES, 2 * COLS], U8, align_bytes=64)
+        x_words = const.tile([P, PASSES, ROWS], U32, align_bytes=64)
+        x_scales = const.tile([P, PASSES, ROWS], U8, align_bytes=64)
+        bias_row = const.tile([P, HALF], BF16)
+        bias_spread = const.tile([P, HALF], BF16)
+        bias_rows = const.tile([P, P], BF16)
+        bias_column = const.tile([P, COLS // P], F32)
         ones = const.tile([P, P], BF16)
-        ident = const.tile([P, P], F32)
-        identb = const.tile([P, P], BF16)
-        rzs = [const.tile([P, 2, JC], F32, name="rz%d" % i) for i in range(NRZ)]
+        identity = const.tile([P, P], F32)
+        identity_bf16 = const.tile([P, P], BF16)
+        folded = [const.tile([P, 2, CHUNK], F32, name="folded%d" % i) for i in range(ZERO_PLANE_TILES)]
 
-        nc.vector.memset(ws[:].bitcast(I32), 0)
-        nc.vector.memset(biasrow[:].bitcast(I32), 0)
-        nc.vector.memset(brows[:].bitcast(I32), 0)
-        make_identity(nc, ident[:])
-        make_identity(nc, identb[:])
+        nc.vector.memset(w_scales[:].bitcast(I32), 0)
+        nc.vector.memset(bias_row[:].bitcast(I32), 0)
+        nc.vector.memset(bias_rows[:].bitcast(I32), 0)
+        make_identity(nc, identity[:])
+        make_identity(nc, identity_bf16[:])
         nc.gpsimd.memset(ones[:], 1.0)
-        for rz in rzs:
-            nc.gpsimd.memset(rz[:, 1, :], 0.0)
+        for tile in folded:
+            nc.gpsimd.memset(tile[:, 1, :], 0.0)
 
-        xins = {}
+        x_in = {}
 
         def load_x(bt):
-            xin = xin_pool.tile([P, 2 * K], BF16)
-            nc.sync.dma_start(out=xin[:], in_=in_data[P * bt : P * (bt + 1), :])
-            xins[bt] = xin
+            x_in[bt] = xin_pool.tile([P, 2 * K], BF16, name="x_in")
+            nc.sync.dma_start(out=x_in[bt][:], in_=in_data[P * bt : P * (bt + 1), :])
 
-        def load_w(half):
-            for g in range(G):
-                a = 2 * HALF * half
+        def load_w_words(half):
+            first_byte = 2 * HALF * half
+            for g in range(PASSES):
                 nc.sync.dma_start(
-                    out=wq[:, g, a : a + 2 * HALF].bitcast(I32),
-                    in_=W_words[g, :, a : a + 2 * HALF].bitcast(I32),
+                    out=w_words[:, g, first_byte : first_byte + 2 * HALF].bitcast(I32),
+                    in_=W_words[g, :, first_byte : first_byte + 2 * HALF].bitcast(I32),
                 )
 
         load_x(0)
-        for g in range(G):
-            for b2 in range(2):
-                for r in range(4):
-                    nc.sync.dma_start(
-                        out=ws[32 * b2 + r : P : 64, g, :].bitcast(I32),
-                        in_=W_scales[g, 4 * b2 + r : 16 : 8, :].bitcast(I32),
-                    )
-        nc.scalar.dma_start(out=biasrow[0:1, :], in_=bias[0:HALF].rearrange("(o n) -> o n", o=1))
-        nc.scalar.dma_start(out=brows[0 : N // P, :], in_=bias.rearrange("(t p) -> t p", p=P))
-        load_w(0)
-        for bt in range(1, 4):
+        for g in range(PASSES):
+            for q in range(8):
+                partition = 32 * (q // 4) + q % 4
+                nc.sync.dma_start(
+                    out=w_scales[partition : P : 64, g, :].bitcast(I32),
+                    in_=W_scales[g, q : 16 : 8, :].bitcast(I32),
+                )
+        nc.scalar.dma_start(out=bias_row[0:1, :], in_=bias[0:HALF].rearrange("(o n) -> o n", o=1))
+        nc.scalar.dma_start(out=bias_rows[0 : COLS // P, :], in_=bias.rearrange("(c p) -> c p", p=P))
+        load_w_words(0)
+        for bt in range(1, TILES_MOVING):
             load_x(bt)
-        load_w(1)
-        for bt in range(4, NB):
+        load_w_words(1)
+        for bt in range(TILES_MOVING, ROW_TILES):
             load_x(bt)
 
-        xcs = {}
-        tps = {}
-        grps = {}
+        x_sorted = {}
+        x_grouped = {}
 
-        def sort(bt):
-            xc = xc_pool.tile([P, K], BF16)
-            imag = xins[bt][:, 1 : 2 * K : 2].rearrange("b (g p u e) -> b g u p e", g=G, p=P, u=2, e=2)
-            dst = xc[:].rearrange("b (g u p e) -> b g u p e", g=G, u=2, p=P, e=2)
-            for g in range(G):
-                if SORT[bt] == "v":
+        def sort_x(bt):
+            x_sorted[bt] = sorted_pool.tile([P, K], BF16, name="x_sorted")
+            imag = x_in[bt][:, 1 : 2 * K : 2].rearrange("b (g p u e) -> b g u p e", g=PASSES, p=P, u=2, e=2)
+            dst = x_sorted[bt][:].rearrange("b (g u p e) -> b g u p e", g=PASSES, u=2, p=P, e=2)
+            for g in range(PASSES):
+                if bt == 0:
                     nc.vector.tensor_copy(out=dst[:, g], in_=imag[:, g])
-                elif SORT[bt] == "s":
+                elif bt in (1, 3):
                     nc.scalar.copy(out=dst[:, g], in_=imag[:, g])
                 else:
                     nc.gpsimd.tensor_scalar(
                         out=dst[:, g], in0=imag[:, g], scalar1=1.0, scalar2=0.0, op0=ALU.mult, op1=ALU.add
                     )
-            xcs[bt] = xc
 
-        def turn(bt):
-            words = xcs[bt][:].bitcast(F32)
-            tp = mxps.tile([P, 2 * G, P], F32, tag="mx")
-            for gu in range(2 * G):
-                nc.tensor.transpose(tp[:, gu, :], words[:, P * gu : P * (gu + 1)], ident[:])
-            grp = grp_pool.tile([P, 4 * G * P], BF16, align_bytes=64)
+        def transpose_x(bt):
+            words = x_sorted[bt][:].bitcast(F32)
+            turned = sums_pool.tile([P, 2 * PASSES, P], F32, tag="sums")
+            for gu in range(2 * PASSES):
+                nc.tensor.transpose(turned[:, gu, :], words[:, P * gu : P * (gu + 1)], identity[:])
+            x_grouped[bt] = grouped_pool.tile([P, PASSES * P * 4], BF16, name="x_grouped", align_bytes=64)
             nc.scalar.copy(
-                out=grp[:].bitcast(F32).rearrange("p (g b u) -> p g b u", g=G, b=P, u=2),
-                in_=tp[:].rearrange("p (g u) b -> p g b u", g=G, u=2),
+                out=x_grouped[bt][:].bitcast(F32).rearrange("p (g b u) -> p g b u", g=PASSES, b=P, u=2),
+                in_=turned[:].rearrange("p (g u) b -> p g b u", g=PASSES, u=2),
             )
-            grps[bt] = grp
 
-        def quant(bt):
-            for g in range(G):
+        def quantise_x(bt):
+            rows = slice(P * bt, P * (bt + 1))
+            for g in range(PASSES):
                 nc.vector.quantize_mx(
-                    out=xq[:, g, P * bt : P * (bt + 1)].bitcast(FP8X4),
-                    scales=xs[:, g, P * bt : P * (bt + 1)],
-                    in_=grps[bt][:, 4 * P * g : 4 * P * (g + 1)],
+                    out=x_words[:, g, rows].bitcast(FP8X4),
+                    scales=x_scales[:, g, rows],
+                    in_=x_grouped[bt][:, 4 * P * g : 4 * P * (g + 1)],
                 )
 
-        def spread_bias(c, eng):
-            ps = mxps.tile([P, JC], F32, tag="mx")
-            nc.tensor.matmul(out=ps[:], lhsT=ones[:], rhs=biasrow[:, JC * c : JC * (c + 1)], start=True, stop=True)
-            if eng == "v":
-                nc.vector.tensor_copy(out=bias_bc[:, JC * c : JC * (c + 1)], in_=ps[:])
+        def spread_bias(jc, engine):
+            cols = slice(CHUNK * jc, CHUNK * (jc + 1))
+            spread = sums_pool.tile([P, CHUNK], F32, tag="sums")
+            nc.tensor.matmul(out=spread[:], lhsT=ones[:], rhs=bias_row[:, cols], start=True, stop=True)
+            if engine == "vector":
+                nc.vector.tensor_copy(out=bias_spread[:, cols], in_=spread[:])
             else:
-                nc.scalar.copy(out=bias_bc[:, JC * c : JC * (c + 1)], in_=ps[:])
+                nc.scalar.copy(out=bias_spread[:, cols], in_=spread[:])
 
-        n1s = {}
+        def bias_onto_partitions():
+            turned = sums_pool.tile([P, P], F32, tag="sums")
+            nc.tensor.matmul(out=turned[:], lhsT=bias_rows[:], rhs=identity_bf16[:], start=True, stop=True)
+            nc.vector.tensor_copy(out=bias_column[:], in_=turned[:, 0 : COLS // P])
+
+        first = {}
 
         def first_half(bt, jc):
-            n0 = JC * jc
-            ps = mxps.tile([P, JC], F32, tag="mx")
-            for g in range(G):
+            rows = slice(P * bt, P * (bt + 1))
+            n0 = CHUNK * jc
+            sums = sums_pool.tile([P, CHUNK], F32, tag="sums")
+            for g in range(PASSES):
                 nc.tensor.matmul_mx(
-                    out=ps[:],
-                    lhsT=xq[:, g, P * bt : P * (bt + 1)].bitcast(FP8X4),
-                    lhsT_scale=xs[:, g, P * bt : P * (bt + 1)],
-                    rhs=wq[:, g, 2 * n0 : 2 * (n0 + JC)].bitcast(FP4X4),
-                    rhs_scale=ws[:, g, n0 : n0 + JC],
+                    out=sums[:],
+                    lhsT=x_words[:, g, rows].bitcast(FP8X4),
+                    lhsT_scale=x_scales[:, g, rows],
+                    rhs=w_words[:, g, 2 * n0 : 2 * (n0 + CHUNK)].bitcast(FP4X4),
+                    rhs_scale=w_scales[:, g, n0 : n0 + CHUNK],
                     start=(g == 0),
-                    stop=(g == G - 1),
+                    stop=(g == PASSES - 1),
                 )
-            n1 = n1_pool.tile([P, JC], F32)
-            nc.vector.tensor_tensor(out=n1[:], in0=ps[:], in1=bias_bc[:, n0 : n0 + JC], op=ALU.add)
-            n1s[(bt, jc)] = n1
+            first[(bt, jc)] = first_pool.tile([P, CHUNK], F32, name="first")
+            nc.vector.tensor_tensor(
+                out=first[(bt, jc)][:], in0=sums[:], in1=bias_spread[:, n0 : n0 + CHUNK], op=ALU.add
+            )
 
         def second_half(h, jc, jt):
-            n0 = HALF + JC * jc + P * jt
-            ps = mxps.tile([P, JC], F32, tag="mx")
-            for g in range(G):
+            rows = slice(CHUNK * h, CHUNK * (h + 1))
+            n0 = HALF + CHUNK * jc + P * jt
+            sums = sums_pool.tile([P, CHUNK], F32, tag="sums")
+            for g in range(PASSES):
                 nc.tensor.matmul_mx(
-                    out=ps[:],
-                    lhsT=wq[:, g, 2 * n0 : 2 * (n0 + P)].bitcast(FP4X4),
-                    lhsT_scale=ws[:, g, n0 : n0 + P],
-                    rhs=xq[:, g, JC * h : JC * (h + 1)].bitcast(FP8X4),
-                    rhs_scale=xs[:, g, JC * h : JC * (h + 1)],
+                    out=sums[:],
+                    lhsT=w_words[:, g, 2 * n0 : 2 * (n0 + P)].bitcast(FP4X4),
+                    lhsT_scale=w_scales[:, g, n0 : n0 + P],
+                    rhs=x_words[:, g, rows].bitcast(FP8X4),
+                    rhs_scale=x_scales[:, g, rows],
                     start=(g == 0),
-                    stop=(g == G - 1),
+                    stop=(g == PASSES - 1),
                 )
-            rbt = rbt_pool.tile([P, JC], F32)
-            nc.scalar.activation(out=rbt[:], in_=ps[:], func=ACT.Relu, bias=bias_t[:, n0 // P : n0 // P + 1], scale=1.0)
-            return rbt
-
-        def turn_back(rbts, i):
-            tb = tbps.tile([P, JC], F32)
-            for jt in range(4):
-                nc.tensor.transpose(tb[:, P * jt : P * (jt + 1)], rbts[jt][:, P * i : P * (i + 1)], ident[:])
-            return tb
-
-        counter = [0]
-
-        def finish(bt, jc, tb):
-            u = counter[0]
-            counter[0] = u + 1
-            rz = rzs[u % NRZ]
-            nc.vector.scalar_tensor_tensor(
-                out=rz[:, 0, :], in0=n1s[(bt, jc)][:], scalar=0.0, in1=tb[:], op0=ALU.max, op1=ALU.subtract
+            second = second_pool.tile([P, CHUNK], F32)
+            nc.scalar.activation(
+                out=second[:], in_=sums[:], func=ACT.Relu, bias=bias_column[:, n0 // P : n0 // P + 1], scale=1.0
             )
-            ot = outp.tile([P, 2 * JC], F32)
-            pairs = ot[:].rearrange("p (j e) -> p j e", e=2)
-            planes = rz[:].rearrange("p e j -> p j e")
-            if IL[u] == "s":
-                nc.scalar.copy(out=pairs, in_=planes)
-            elif IL[u] == "g":
-                nc.gpsimd.tensor_scalar(out=pairs, in0=planes, scalar1=1.0, scalar2=0.0, op0=ALU.mult, op1=ALU.add)
-            else:
-                nc.vector.tensor_copy(out=pairs, in_=planes)
-            nc.sync.dma_start(out=out2[P * bt : P * (bt + 1), 2 * JC * jc : 2 * JC * (jc + 1)], in_=ot[:])
+            return second
 
-        sort(0)
-        turn(0)
-        quant(0)
-        spread_bias(0, "v")
-        for c in range(1, NJ):
-            spread_bias(c, "s")
-        pst = mxps.tile([P, P], F32, tag="mx")
-        nc.tensor.matmul(out=pst[:], lhsT=brows[:], rhs=identb[:], start=True, stop=True)
-        nc.vector.tensor_copy(out=bias_t[:], in_=pst[:, 0 : N // P])
-        sort(2)
-        for jc in range(NJ):
-            first_half(0, jc)
-        sort(1)
-        turn(1)
-        quant(1)
-        sort(3)
-        first_half(1, 0)
-        turn(2)
-        quant(2)
-        first_half(1, 1)
-        turn(3)
-        quant(3)
-        first_half(2, 0)
-        first_half(3, 0)
-        groups = {}
-        for q in range(9):
-            h, jc = q // NJ, q % NJ
-            if q == 0:
-                for bt in range(4, NB):
-                    sort(bt)
-            if q < 8:
-                rbts = [second_half(h, jc, jt) for jt in range(4)]
-            if q >= 1:
-                ph, pjc, tbs = groups[q - 1]
-                for i in range(4):
-                    finish(4 * ph + i, pjc, tbs[i])
-            if q < 8:
-                for bt, j in PLAN[q]:
-                    first_half(bt, j)
-                groups[q] = (h, jc, [turn_back(rbts, i) for i in range(4)])
-            if q < 2:
-                turn(4 + 2 * q)
-                turn(5 + 2 * q)
-                quant(4 + 2 * q)
-                quant(5 + 2 * q)
+        def transpose_back(seconds, i):
+            back = back_pool.tile([P, CHUNK], F32)
+            for jt in range(TILES_MOVING):
+                nc.tensor.transpose(back[:, P * jt : P * (jt + 1)], seconds[jt][:, P * i : P * (i + 1)], identity[:])
+            return back
+
+        def finish(unit, bt, jc, back):
+            planes = folded[unit % ZERO_PLANE_TILES]
+            nc.vector.scalar_tensor_tensor(
+                out=planes[:, 0, :], in0=first[(bt, jc)][:], scalar=0.0, in1=back[:], op0=ALU.max, op1=ALU.subtract
+            )
+            store = store_pool.tile([P, 2 * CHUNK], F32)
+            pairs = store[:].rearrange("p (j e) -> p j e", e=2)
+            alternately = planes[:].rearrange("p e j -> p j e")
+            if unit % 2 == 0:
+                nc.gpsimd.tensor_scalar(
+                    out=pairs, in0=alternately, scalar1=1.0, scalar2=0.0, op0=ALU.mult, op1=ALU.add
+                )
+            else:
+                nc.scalar.copy(out=pairs, in_=alternately)
+            nc.sync.dma_start(
+                out=out_rows[P * bt : P * (bt + 1), 2 * CHUNK * jc : 2 * CHUNK * (jc + 1)], in_=store[:]
+            )
+
+        sort_x(0)
+        transpose_x(0)
+        quantise_x(0)
+        spread_bias(0, "vector")
+        for jc in range(1, CHUNKS):
+            spread_bias(jc, "scalar")
+        bias_onto_partitions()
+        sort_x(2)
+        for unit in LEAD[0:4]:
+            first_half(*unit)
+        sort_x(1)
+        transpose_x(1)
+        quantise_x(1)
+        sort_x(3)
+        first_half(*LEAD[4])
+        transpose_x(2)
+        quantise_x(2)
+        first_half(*LEAD[5])
+        transpose_x(3)
+        quantise_x(3)
+        first_half(*LEAD[6])
+        first_half(*LEAD[7])
+
+        needed = [
+            (TILES_MOVING * h + i, jc)
+            for h in range(ROW_TILES // TILES_MOVING)
+            for jc in range(CHUNKS)
+            for i in range(TILES_MOVING)
+        ]
+        later = [unit for unit in needed if unit not in LEAD]
+
+        backs = {}
+        for bt in range(TILES_MOVING, ROW_TILES):
+            sort_x(bt)
+        for q in range(ROUNDS + 1):
+            h, jc = q // CHUNKS, q % CHUNKS
+            if q < ROUNDS:
+                seconds = [second_half(h, jc, jt) for jt in range(TILES_MOVING)]
+            if q > 0:
+                for i in range(TILES_MOVING):
+                    finish(
+                        TILES_MOVING * (q - 1) + i,
+                        TILES_MOVING * ((q - 1) // CHUNKS) + i,
+                        (q - 1) % CHUNKS,
+                        backs[(q - 1, i)],
+                    )
+            if q < ROUNDS:
+                for unit in later[UNITS_A_ROUND * q : UNITS_A_ROUND * (q + 1)]:
+                    first_half(*unit)
+                for i in range(TILES_MOVING):
+                    backs[(q, i)] = transpose_back(seconds, i)
+            if q < (ROW_TILES - TILES_MOVING) // 2:
+                transpose_x(TILES_MOVING + 2 * q)
+                transpose_x(TILES_MOVING + 2 * q + 1)
+                quantise_x(TILES_MOVING + 2 * q)
+                quantise_x(TILES_MOVING + 2 * q + 1)

@@ -24,8 +24,6 @@ CHUNK = 512
 CHUNKS = HALF // CHUNK
 TILES_MOVING = CHUNK // P
 ROUNDS = (ROW_TILES // TILES_MOVING) * CHUNKS
-LEAD = ((0, 0), (0, 1), (0, 2), (0, 3), (1, 0), (1, 1), (2, 0), (3, 0))
-UNITS_A_ROUND = (ROW_TILES * CHUNKS - len(LEAD)) // ROUNDS
 ZERO_PLANE_TILES = 6
 
 FLOPS = 2 * ROWS * K * COLS
@@ -37,9 +35,9 @@ def tile_middlelayer_kernel(tc, in_data, W_words, W_scales, bias, out):
     with ExitStack() as ctx:
         const = ctx.enter_context(tc.tile_pool(name="const", bufs=1))
         xin_pool = ctx.enter_context(tc.tile_pool(name="xin", bufs=ROW_TILES))
-        sorted_pool = ctx.enter_context(tc.tile_pool(name="sorted", bufs=4))
-        grouped_pool = ctx.enter_context(tc.tile_pool(name="grouped", bufs=3))
-        first_pool = ctx.enter_context(tc.tile_pool(name="first", bufs=24))
+        sorted_pool = ctx.enter_context(tc.tile_pool(name="sorted", bufs=TILES_MOVING))
+        grouped_pool = ctx.enter_context(tc.tile_pool(name="grouped", bufs=TILES_MOVING))
+        first_pool = ctx.enter_context(tc.tile_pool(name="first", bufs=2 * TILES_MOVING))
         second_pool = ctx.enter_context(tc.tile_pool(name="second", bufs=2 * TILES_MOVING))
         store_pool = ctx.enter_context(tc.tile_pool(name="store", bufs=8))
         sums_pool = ctx.enter_context(tc.psum_pool(name="sums", bufs=4))
@@ -74,15 +72,17 @@ def tile_middlelayer_kernel(tc, in_data, W_words, W_scales, bias, out):
             x_in[bt] = xin_pool.tile([P, 2 * K], BF16, name="x_in")
             nc.sync.dma_start(out=x_in[bt][:], in_=in_data[P * bt : P * (bt + 1), :])
 
-        def load_w_words(half):
-            first_byte = 2 * HALF * half
-            for g in range(PASSES):
-                nc.sync.dma_start(
-                    out=w_words[:, g, first_byte : first_byte + 2 * HALF].bitcast(I32),
-                    in_=W_words[g, :, first_byte : first_byte + 2 * HALF].bitcast(I32),
-                )
+        def load_w_words(jc):
+            for half in (1, 0):
+                first_byte = 2 * (HALF * half + CHUNK * jc)
+                for g in range(PASSES):
+                    nc.sync.dma_start(
+                        out=w_words[:, g, first_byte : first_byte + 2 * CHUNK].bitcast(I32),
+                        in_=W_words[g, :, first_byte : first_byte + 2 * CHUNK].bitcast(I32),
+                    )
 
-        load_x(0)
+        for bt in range(TILES_MOVING):
+            load_x(bt)
         for g in range(PASSES):
             for q in range(8):
                 partition = 32 * (q // 4) + q % 4
@@ -93,11 +93,13 @@ def tile_middlelayer_kernel(tc, in_data, W_words, W_scales, bias, out):
         nc.scalar.dma_start(out=bias_row[0:1, :], in_=bias[0:HALF].rearrange("(o n) -> o n", o=1))
         nc.scalar.dma_start(out=bias_rows[0 : COLS // P, :], in_=bias.rearrange("(c p) -> c p", p=P))
         load_w_words(0)
-        for bt in range(1, TILES_MOVING):
-            load_x(bt)
         load_w_words(1)
-        for bt in range(TILES_MOVING, ROW_TILES):
-            load_x(bt)
+        load_x(4)
+        load_x(5)
+        load_w_words(2)
+        load_x(6)
+        load_x(7)
+        load_w_words(3)
 
         x_sorted = {}
         x_grouped = {}
@@ -107,9 +109,9 @@ def tile_middlelayer_kernel(tc, in_data, W_words, W_scales, bias, out):
             imag = x_in[bt][:, 1 : 2 * K : 2].rearrange("b (g p u e) -> b g u p e", g=PASSES, p=P, u=2, e=2)
             dst = x_sorted[bt][:].rearrange("b (g u p e) -> b g u p e", g=PASSES, u=2, p=P, e=2)
             for g in range(PASSES):
-                if bt == 0:
+                if bt in (0, 2, 3):
                     nc.vector.tensor_copy(out=dst[:, g], in_=imag[:, g])
-                elif bt in (1, 3):
+                elif bt == 1:
                     nc.scalar.copy(out=dst[:, g], in_=imag[:, g])
                 else:
                     nc.gpsimd.tensor_scalar(
@@ -136,14 +138,11 @@ def tile_middlelayer_kernel(tc, in_data, W_words, W_scales, bias, out):
                     in_=x_grouped[bt][:, 4 * P * g : 4 * P * (g + 1)],
                 )
 
-        def spread_bias(jc, engine):
+        def spread_bias(jc):
             cols = slice(CHUNK * jc, CHUNK * (jc + 1))
             spread = sums_pool.tile([P, CHUNK], F32, tag="sums")
             nc.tensor.matmul(out=spread[:], lhsT=ones[:], rhs=bias_row[:, cols], start=True, stop=True)
-            if engine == "vector":
-                nc.vector.tensor_copy(out=bias_spread[:, cols], in_=spread[:])
-            else:
-                nc.scalar.copy(out=bias_spread[:, cols], in_=spread[:])
+            nc.scalar.copy(out=bias_spread[:, cols], in_=spread[:])
 
         def bias_onto_partitions():
             turned = sums_pool.tile([P, P], F32, tag="sums")
@@ -197,15 +196,15 @@ def tile_middlelayer_kernel(tc, in_data, W_words, W_scales, bias, out):
                 nc.tensor.transpose(back[:, P * jt : P * (jt + 1)], seconds[jt][:, P * i : P * (i + 1)], identity[:])
             return back
 
-        def finish(unit, bt, jc, back):
-            planes = folded[unit % ZERO_PLANE_TILES]
+        def finish(number, bt, jc, back):
+            planes = folded[number % ZERO_PLANE_TILES]
             nc.vector.scalar_tensor_tensor(
                 out=planes[:, 0, :], in0=first[(bt, jc)][:], scalar=0.0, in1=back[:], op0=ALU.max, op1=ALU.subtract
             )
             store = store_pool.tile([P, 2 * CHUNK], F32)
             pairs = store[:].rearrange("p (j e) -> p j e", e=2)
             alternately = planes[:].rearrange("p e j -> p j e")
-            if unit % 2 == 0:
+            if number % 2 == 0:
                 nc.gpsimd.tensor_scalar(
                     out=pairs, in0=alternately, scalar1=1.0, scalar2=0.0, op0=ALU.mult, op1=ALU.add
                 )
@@ -216,39 +215,21 @@ def tile_middlelayer_kernel(tc, in_data, W_words, W_scales, bias, out):
             )
 
         sort_x(0)
+        sort_x(1)
         transpose_x(0)
-        quantise_x(0)
-        spread_bias(0, "vector")
-        for jc in range(1, CHUNKS):
-            spread_bias(jc, "scalar")
         bias_onto_partitions()
         sort_x(2)
-        for unit in LEAD[0:4]:
-            first_half(*unit)
-        sort_x(1)
         transpose_x(1)
-        quantise_x(1)
         sort_x(3)
-        first_half(*LEAD[4])
         transpose_x(2)
-        quantise_x(2)
-        first_half(*LEAD[5])
+        quantise_x(0)
+        quantise_x(1)
         transpose_x(3)
+        quantise_x(2)
         quantise_x(3)
-        first_half(*LEAD[6])
-        first_half(*LEAD[7])
-
-        needed = [
-            (TILES_MOVING * h + i, jc)
-            for h in range(ROW_TILES // TILES_MOVING)
-            for jc in range(CHUNKS)
-            for i in range(TILES_MOVING)
-        ]
-        later = [unit for unit in needed if unit not in LEAD]
+        spread_bias(0)
 
         backs = {}
-        for bt in range(TILES_MOVING, ROW_TILES):
-            sort_x(bt)
         for q in range(ROUNDS + 1):
             h, jc = q // CHUNKS, q % CHUNKS
             if q < ROUNDS:
@@ -261,13 +242,18 @@ def tile_middlelayer_kernel(tc, in_data, W_words, W_scales, bias, out):
                         (q - 1) % CHUNKS,
                         backs[(q - 1, i)],
                     )
+            if q in (0, 1):
+                sort_x(TILES_MOVING + 2 * q)
+                sort_x(TILES_MOVING + 2 * q + 1)
             if q < ROUNDS:
-                for unit in later[UNITS_A_ROUND * q : UNITS_A_ROUND * (q + 1)]:
-                    first_half(*unit)
+                for i in range(TILES_MOVING):
+                    first_half(TILES_MOVING * h + i, jc)
+                if q + 1 < CHUNKS:
+                    spread_bias(q + 1)
                 for i in range(TILES_MOVING):
                     backs[(q, i)] = transpose_back(seconds, i)
-            if q < (ROW_TILES - TILES_MOVING) // 2:
-                transpose_x(TILES_MOVING + 2 * q)
-                transpose_x(TILES_MOVING + 2 * q + 1)
-                quantise_x(TILES_MOVING + 2 * q)
-                quantise_x(TILES_MOVING + 2 * q + 1)
+            if q in (1, 2):
+                transpose_x(TILES_MOVING + 2 * (q - 1))
+                transpose_x(TILES_MOVING + 2 * (q - 1) + 1)
+                quantise_x(TILES_MOVING + 2 * (q - 1))
+                quantise_x(TILES_MOVING + 2 * (q - 1) + 1)

@@ -94,12 +94,10 @@ def tile_middlelayer_kernel(tc, in_data, W_words, W_scales, bias, out):
         nc.scalar.dma_start(out=bias_rows[0 : COLS // P, :], in_=bias.rearrange("(c p) -> c p", p=P))
         load_w_words(0)
         load_w_words(1)
-        load_x(4)
-        load_x(5)
-        load_w_words(2)
-        load_x(6)
-        load_x(7)
-        load_w_words(3)
+        for jc in range(2, CHUNKS):
+            load_x(2 * jc)
+            load_x(2 * jc + 1)
+            load_w_words(jc)
 
         x_sorted = {}
         x_grouped = {}
@@ -138,11 +136,17 @@ def tile_middlelayer_kernel(tc, in_data, W_words, W_scales, bias, out):
                     in_=x_grouped[bt][:, 4 * P * g : 4 * P * (g + 1)],
                 )
 
+        spreads = {}
+
         def spread_bias(jc):
-            cols = slice(CHUNK * jc, CHUNK * (jc + 1))
-            spread = sums_pool.tile([P, CHUNK], F32, tag="sums")
-            nc.tensor.matmul(out=spread[:], lhsT=ones[:], rhs=bias_row[:, cols], start=True, stop=True)
-            nc.scalar.copy(out=bias_spread[:, cols], in_=spread[:])
+            spreads[jc] = back_pool.tile([P, CHUNK], F32, name="spread", tag="back")
+            nc.tensor.matmul(
+                out=spreads[jc][:],
+                lhsT=ones[:],
+                rhs=bias_row[:, CHUNK * jc : CHUNK * (jc + 1)],
+                start=True,
+                stop=True,
+            )
 
         def bias_onto_partitions():
             turned = sums_pool.tile([P, P], F32, tag="sums")
@@ -191,7 +195,7 @@ def tile_middlelayer_kernel(tc, in_data, W_words, W_scales, bias, out):
             return second
 
         def transpose_back(seconds, i):
-            back = back_pool.tile([P, CHUNK], F32)
+            back = back_pool.tile([P, CHUNK], F32, tag="back")
             for jt in range(TILES_MOVING):
                 nc.tensor.transpose(back[:, P * jt : P * (jt + 1)], seconds[jt][:, P * i : P * (i + 1)], identity[:])
             return back
@@ -218,16 +222,22 @@ def tile_middlelayer_kernel(tc, in_data, W_words, W_scales, bias, out):
         sort_x(1)
         transpose_x(0)
         bias_onto_partitions()
+        spread_bias(0)
         sort_x(2)
         transpose_x(1)
+        spread_bias(1)
         sort_x(3)
         transpose_x(2)
+        spread_bias(2)
         quantise_x(0)
         quantise_x(1)
         transpose_x(3)
+        spread_bias(3)
         quantise_x(2)
         quantise_x(3)
-        spread_bias(0)
+        nc.scalar.copy(out=bias_spread[:, 0:CHUNK], in_=spreads[0][:])
+        for jc in range(1, CHUNKS):
+            nc.vector.tensor_copy(out=bias_spread[:, CHUNK * jc : CHUNK * (jc + 1)], in_=spreads[jc][:])
 
         backs = {}
         for q in range(ROUNDS + 1):
@@ -248,8 +258,6 @@ def tile_middlelayer_kernel(tc, in_data, W_words, W_scales, bias, out):
             if q < ROUNDS:
                 for i in range(TILES_MOVING):
                     first_half(TILES_MOVING * h + i, jc)
-                if q + 1 < CHUNKS:
-                    spread_bias(q + 1)
                 for i in range(TILES_MOVING):
                     backs[(q, i)] = transpose_back(seconds, i)
             if q in (1, 2):

@@ -26,7 +26,10 @@ TILES_MOVING = CHUNK // P
 ROUNDS = (ROW_TILES // TILES_MOVING) * CHUNKS
 ZERO_PLANE_TILES = 6
 
+W_LOAD = 2 * CHUNK
 FLOPS = 2 * ROWS * K * COLS
+USUAL = "GGGS"
+LAST = "GSGS"
 
 
 def tile_middlelayer_kernel(tc, in_data, W_words, W_scales, bias, out):
@@ -37,15 +40,17 @@ def tile_middlelayer_kernel(tc, in_data, W_words, W_scales, bias, out):
         xin_pool = ctx.enter_context(tc.tile_pool(name="xin", bufs=ROW_TILES))
         sorted_pool = ctx.enter_context(tc.tile_pool(name="sorted", bufs=TILES_MOVING))
         grouped_pool = ctx.enter_context(tc.tile_pool(name="grouped", bufs=TILES_MOVING))
-        first_pool = ctx.enter_context(tc.tile_pool(name="first", bufs=2 * TILES_MOVING))
+        first_pool = ctx.enter_context(tc.tile_pool(name="first", bufs=16))
         second_pool = ctx.enter_context(tc.tile_pool(name="second", bufs=2 * TILES_MOVING))
-        store_pool = ctx.enter_context(tc.tile_pool(name="store", bufs=8))
+        store_pool = ctx.enter_context(tc.tile_pool(name="store", bufs=12))
         sums_pool = ctx.enter_context(tc.psum_pool(name="sums", bufs=4))
         back_pool = ctx.enter_context(tc.psum_pool(name="back", bufs=TILES_MOVING))
         ctx.enter_context(tc.manual_schedule())
 
         w_scales = const.tile([P, PASSES, COLS], U8, align_bytes=64)
-        w_words = const.tile([P, PASSES, 2 * COLS], U8, align_bytes=64)
+        w_words = [
+            const.tile([P, PASSES, 2 * W_LOAD], U8, align_bytes=64, name="w_words%d" % i) for i in range(COLS // W_LOAD)
+        ]
         x_words = const.tile([P, PASSES, ROWS], U32, align_bytes=64)
         x_scales = const.tile([P, PASSES, ROWS], U8, align_bytes=64)
         bias_row = const.tile([P, HALF], BF16)
@@ -58,13 +63,11 @@ def tile_middlelayer_kernel(tc, in_data, W_words, W_scales, bias, out):
         folded = [const.tile([P, 2, CHUNK], F32, name="folded%d" % i) for i in range(ZERO_PLANE_TILES)]
 
         nc.vector.memset(w_scales[:].bitcast(I32), 0)
-        nc.vector.memset(bias_row[:].bitcast(I32), 0)
-        nc.vector.memset(bias_rows[:].bitcast(I32), 0)
+        nc.gpsimd.memset(bias_rows[:].bitcast(F32), 0.0)
+        nc.gpsimd.memset(bias_row[:].bitcast(F32), 0.0)
         make_identity(nc, identity[:])
         make_identity(nc, identity_bf16[:])
         nc.gpsimd.memset(ones[:], 1.0)
-        for tile in folded:
-            nc.gpsimd.memset(tile[:, 1, :], 0.0)
 
         x_in = {}
 
@@ -72,32 +75,37 @@ def tile_middlelayer_kernel(tc, in_data, W_words, W_scales, bias, out):
             x_in[bt] = xin_pool.tile([P, 2 * K], BF16, name="x_in")
             nc.sync.dma_start(out=x_in[bt][:], in_=in_data[P * bt : P * (bt + 1), :])
 
-        def load_w_words(jc):
-            for half in (1, 0):
-                first_byte = 2 * (HALF * half + CHUNK * jc)
-                for g in range(PASSES):
-                    nc.sync.dma_start(
-                        out=w_words[:, g, first_byte : first_byte + 2 * CHUNK].bitcast(I32),
-                        in_=W_words[g, :, first_byte : first_byte + 2 * CHUNK].bitcast(I32),
-                    )
+        def load_w_words(half, pair):
+            i = (HALF // W_LOAD) * half + pair
+            nc.sync.dma_start(
+                out=w_words[i][:].bitcast(I32),
+                in_=W_words[:, :, 2 * W_LOAD * i : 2 * W_LOAD * (i + 1)].rearrange("g p n -> p g n").bitcast(I32),
+            )
 
-        for bt in range(TILES_MOVING):
-            load_x(bt)
-        for g in range(PASSES):
-            for q in range(8):
-                partition = 32 * (q // 4) + q % 4
-                nc.sync.dma_start(
-                    out=w_scales[partition : P : 64, g, :].bitcast(I32),
-                    in_=W_scales[g, q : 16 : 8, :].bitcast(I32),
-                )
+        def w_columns(g, n0, width):
+            first_byte = 2 * (n0 % W_LOAD)
+            return w_words[n0 // W_LOAD][:, g, first_byte : first_byte + 2 * width].bitcast(FP4X4)
+
+        load_x(0)
+        load_x(1)
+        for r in range(4):
+            nc.sync.dma_start(
+                out=w_scales[r : P : 32, :, :].bitcast(I32),
+                in_=W_scales[:, r : 16 : 4, :].rearrange("g q n -> q g n").bitcast(I32),
+            )
         nc.scalar.dma_start(out=bias_row[0:1, :], in_=bias[0:HALF].rearrange("(o n) -> o n", o=1))
         nc.scalar.dma_start(out=bias_rows[0 : COLS // P, :], in_=bias.rearrange("(c p) -> c p", p=P))
-        load_w_words(0)
-        load_w_words(1)
-        for jc in range(2, CHUNKS):
-            load_x(2 * jc)
-            load_x(2 * jc + 1)
-            load_w_words(jc)
+        load_w_words(0, 0)
+        load_x(2)
+        load_x(3)
+        load_w_words(0, 1)
+        load_w_words(1, 0)
+        load_x(4)
+        load_x(5)
+        load_w_words(1, 1)
+        load_x(6)
+        load_x(7)
+
 
         x_sorted = {}
         x_grouped = {}
@@ -107,10 +115,8 @@ def tile_middlelayer_kernel(tc, in_data, W_words, W_scales, bias, out):
             imag = x_in[bt][:, 1 : 2 * K : 2].rearrange("b (g p u e) -> b g u p e", g=PASSES, p=P, u=2, e=2)
             dst = x_sorted[bt][:].rearrange("b (g u p e) -> b g u p e", g=PASSES, u=2, p=P, e=2)
             for g in range(PASSES):
-                if bt in (0, 2, 3):
+                if bt in (0, 1) or (bt in (2, 3) and g == 0):
                     nc.vector.tensor_copy(out=dst[:, g], in_=imag[:, g])
-                elif bt == 1:
-                    nc.scalar.copy(out=dst[:, g], in_=imag[:, g])
                 else:
                     nc.gpsimd.tensor_scalar(
                         out=dst[:, g], in0=imag[:, g], scalar1=1.0, scalar2=0.0, op0=ALU.mult, op1=ALU.add
@@ -155,16 +161,19 @@ def tile_middlelayer_kernel(tc, in_data, W_words, W_scales, bias, out):
 
         first = {}
 
-        def first_half(bt, jc):
+        def first_half(bt, jc, spare_bank=False):
             rows = slice(P * bt, P * (bt + 1))
             n0 = CHUNK * jc
-            sums = sums_pool.tile([P, CHUNK], F32, tag="sums")
+            if spare_bank:
+                sums = back_pool.tile([P, CHUNK], F32, tag="back")
+            else:
+                sums = sums_pool.tile([P, CHUNK], F32, tag="sums")
             for g in range(PASSES):
                 nc.tensor.matmul_mx(
                     out=sums[:],
                     lhsT=x_words[:, g, rows].bitcast(FP8X4),
                     lhsT_scale=x_scales[:, g, rows],
-                    rhs=w_words[:, g, 2 * n0 : 2 * (n0 + CHUNK)].bitcast(FP4X4),
+                    rhs=w_columns(g, n0, CHUNK),
                     rhs_scale=w_scales[:, g, n0 : n0 + CHUNK],
                     start=(g == 0),
                     stop=(g == PASSES - 1),
@@ -181,7 +190,7 @@ def tile_middlelayer_kernel(tc, in_data, W_words, W_scales, bias, out):
             for g in range(PASSES):
                 nc.tensor.matmul_mx(
                     out=sums[:],
-                    lhsT=w_words[:, g, 2 * n0 : 2 * (n0 + P)].bitcast(FP4X4),
+                    lhsT=w_columns(g, n0, P),
                     lhsT_scale=w_scales[:, g, n0 : n0 + P],
                     rhs=x_words[:, g, rows].bitcast(FP8X4),
                     rhs_scale=x_scales[:, g, rows],
@@ -208,37 +217,58 @@ def tile_middlelayer_kernel(tc, in_data, W_words, W_scales, bias, out):
             store = store_pool.tile([P, 2 * CHUNK], F32)
             pairs = store[:].rearrange("p (j e) -> p j e", e=2)
             alternately = planes[:].rearrange("p e j -> p j e")
-            if number % 2 == 0:
+            engine = (LAST if number >= 28 else USUAL)[number % 4]
+            if engine == "G":
                 nc.gpsimd.tensor_scalar(
                     out=pairs, in0=alternately, scalar1=1.0, scalar2=0.0, op0=ALU.mult, op1=ALU.add
                 )
-            else:
+            elif engine == "S":
                 nc.scalar.copy(out=pairs, in_=alternately)
+            else:
+                nc.vector.tensor_copy(out=pairs, in_=alternately)
             nc.sync.dma_start(
                 out=out_rows[P * bt : P * (bt + 1), 2 * CHUNK * jc : 2 * CHUNK * (jc + 1)], in_=store[:]
             )
 
+        def copy_spread(jc):
+            nc.scalar.copy(out=bias_spread[:, CHUNK * jc : CHUNK * (jc + 1)], in_=spreads[jc][:])
+
         sort_x(0)
-        sort_x(1)
         transpose_x(0)
+        sort_x(1)
         bias_onto_partitions()
         spread_bias(0)
-        sort_x(2)
-        transpose_x(1)
+        copy_spread(0)
         spread_bias(1)
-        sort_x(3)
-        transpose_x(2)
-        spread_bias(2)
         quantise_x(0)
+        transpose_x(1)
+        copy_spread(1)
+        sort_x(2)
         quantise_x(1)
-        transpose_x(3)
+        first_half(0, 0)
+        sort_x(3)
+        first_half(0, 1)
+        spread_bias(2)
+        copy_spread(2)
         spread_bias(3)
+        copy_spread(3)
+        first_half(1, 0)
+        first_half(1, 1)
+        transpose_x(2)
+        transpose_x(3)
         quantise_x(2)
         quantise_x(3)
-        nc.scalar.copy(out=bias_spread[:, 0:CHUNK], in_=spreads[0][:])
-        for jc in range(1, CHUNKS):
-            nc.vector.tensor_copy(out=bias_spread[:, CHUNK * jc : CHUNK * (jc + 1)], in_=spreads[jc][:])
+        first_half(0, 2, True)
+        first_half(0, 3, True)
+        first_half(1, 2, True)
+        first_half(1, 3, True)
+        for tile in folded:
+            nc.gpsimd.memset(tile[:, 1, :], 0.0)
+        for bt in range(TILES_MOVING, ROW_TILES):
+            sort_x(bt)
 
+        fillers = [(bt, jc) for jc in range(CHUNKS) for bt in (2, 3)]
+        fillers += [(bt, jc) for jc in range(CHUNKS) for bt in range(TILES_MOVING, ROW_TILES)]
         backs = {}
         for q in range(ROUNDS + 1):
             h, jc = q // CHUNKS, q % CHUNKS
@@ -252,16 +282,12 @@ def tile_middlelayer_kernel(tc, in_data, W_words, W_scales, bias, out):
                         (q - 1) % CHUNKS,
                         backs[(q - 1, i)],
                     )
-            if q in (0, 1):
-                sort_x(TILES_MOVING + 2 * q)
-                sort_x(TILES_MOVING + 2 * q + 1)
             if q < ROUNDS:
-                for i in range(TILES_MOVING):
-                    first_half(TILES_MOVING * h + i, jc)
+                for bt, chunk in fillers[3 * q : 3 * q + 3]:
+                    first_half(bt, chunk)
                 for i in range(TILES_MOVING):
                     backs[(q, i)] = transpose_back(seconds, i)
-            if q in (1, 2):
-                transpose_x(TILES_MOVING + 2 * (q - 1))
-                transpose_x(TILES_MOVING + 2 * (q - 1) + 1)
-                quantise_x(TILES_MOVING + 2 * (q - 1))
-                quantise_x(TILES_MOVING + 2 * (q - 1) + 1)
+            if q < 2:
+                for bt in (TILES_MOVING + 2 * q, TILES_MOVING + 2 * q + 1):
+                    transpose_x(bt)
+                    quantise_x(bt)

@@ -28,8 +28,9 @@ ZERO_PLANE_TILES = 6
 
 W_LOAD = 2 * CHUNK
 FLOPS = 2 * ROWS * K * COLS
-USUAL = "GGGS"
-LAST = "GSGS"
+USUAL = "GSSV"
+LAST = "SGSVSGSV"
+FILL = (3, 3, 3, 3, 3, 3, 3, 3)
 
 
 def tile_middlelayer_kernel(tc, in_data, W_words, W_scales, bias, out):
@@ -117,6 +118,8 @@ def tile_middlelayer_kernel(tc, in_data, W_words, W_scales, bias, out):
             for g in range(PASSES):
                 if bt in (0, 1) or (bt in (2, 3) and g == 0):
                     nc.vector.tensor_copy(out=dst[:, g], in_=imag[:, g])
+                elif bt in (2, 3):
+                    nc.scalar.copy(out=dst[:, g], in_=imag[:, g])
                 else:
                     nc.gpsimd.tensor_scalar(
                         out=dst[:, g], in0=imag[:, g], scalar1=1.0, scalar2=0.0, op0=ALU.mult, op1=ALU.add
@@ -203,21 +206,26 @@ def tile_middlelayer_kernel(tc, in_data, W_words, W_scales, bias, out):
             )
             return second
 
-        def transpose_back(seconds, i):
-            back = back_pool.tile([P, CHUNK], F32, tag="back")
-            for jt in range(TILES_MOVING):
-                nc.tensor.transpose(back[:, P * jt : P * (jt + 1)], seconds[jt][:, P * i : P * (i + 1)], identity[:])
+        def transpose_back(seconds, i, tiles=(0, 1, 2, 3), spare_bank=False):
+            if spare_bank:
+                back = sums_pool.tile([P, P * len(tiles)], F32, tag="sums")
+            else:
+                back = back_pool.tile([P, P * len(tiles)], F32, tag="back")
+            for n, jt in enumerate(tiles):
+                nc.tensor.transpose(back[:, P * n : P * (n + 1)], seconds[jt][:, P * i : P * (i + 1)], identity[:])
             return back
 
-        def finish(number, bt, jc, back):
+        def fold(number, bt, jc, back, j0=0, width=CHUNK):
             planes = folded[number % ZERO_PLANE_TILES]
             nc.vector.scalar_tensor_tensor(
-                out=planes[:, 0, :], in0=first[(bt, jc)][:], scalar=0.0, in1=back[:], op0=ALU.max, op1=ALU.subtract
+                out=planes[:, 0, 0:width], in0=first[(bt, jc)][:, j0 : j0 + width], scalar=0.0, in1=back[:], op0=ALU.max, op1=ALU.subtract
             )
-            store = store_pool.tile([P, 2 * CHUNK], F32)
+
+        def store_unit(number, bt, jc, engine, j0=0, width=CHUNK):
+            planes = folded[number % ZERO_PLANE_TILES]
+            store = store_pool.tile([P, 2 * width], F32, name="store")
             pairs = store[:].rearrange("p (j e) -> p j e", e=2)
-            alternately = planes[:].rearrange("p e j -> p j e")
-            engine = (LAST if number >= 28 else USUAL)[number % 4]
+            alternately = planes[:, :, 0:width].rearrange("p e j -> p j e")
             if engine == "G":
                 nc.gpsimd.tensor_scalar(
                     out=pairs, in0=alternately, scalar1=1.0, scalar2=0.0, op0=ALU.mult, op1=ALU.add
@@ -227,7 +235,7 @@ def tile_middlelayer_kernel(tc, in_data, W_words, W_scales, bias, out):
             else:
                 nc.vector.tensor_copy(out=pairs, in_=alternately)
             nc.sync.dma_start(
-                out=out_rows[P * bt : P * (bt + 1), 2 * CHUNK * jc : 2 * CHUNK * (jc + 1)], in_=store[:]
+                out=out_rows[P * bt : P * (bt + 1), 2 * (CHUNK * jc + j0) : 2 * (CHUNK * jc + j0 + width)], in_=store[:]
             )
 
         def copy_spread(jc):
@@ -243,8 +251,8 @@ def tile_middlelayer_kernel(tc, in_data, W_words, W_scales, bias, out):
         quantise_x(0)
         transpose_x(1)
         copy_spread(1)
-        sort_x(2)
         quantise_x(1)
+        sort_x(2)
         first_half(0, 0)
         sort_x(3)
         first_half(0, 1)
@@ -269,25 +277,31 @@ def tile_middlelayer_kernel(tc, in_data, W_words, W_scales, bias, out):
 
         fillers = [(bt, jc) for jc in range(CHUNKS) for bt in (2, 3)]
         fillers += [(bt, jc) for jc in range(CHUNKS) for bt in range(TILES_MOVING, ROW_TILES)]
-        backs = {}
-        for q in range(ROUNDS + 1):
+        taken = 0
+        for q in range(ROUNDS):
             h, jc = q // CHUNKS, q % CHUNKS
-            if q < ROUNDS:
-                seconds = [second_half(h, jc, jt) for jt in range(TILES_MOVING)]
+            seconds = [second_half(h, jc, jt) for jt in range(TILES_MOVING)]
             if q > 0:
                 for i in range(TILES_MOVING):
-                    finish(
-                        TILES_MOVING * (q - 1) + i,
-                        TILES_MOVING * ((q - 1) // CHUNKS) + i,
-                        (q - 1) % CHUNKS,
-                        backs[(q - 1, i)],
-                    )
-            if q < ROUNDS:
-                for bt, chunk in fillers[3 * q : 3 * q + 3]:
-                    first_half(bt, chunk)
+                    if USUAL[i] == "S":
+                        store_unit(TILES_MOVING * (q - 1) + i, TILES_MOVING * ((q - 1) // CHUNKS) + i, (q - 1) % CHUNKS, "S")
+            for bt, chunk in fillers[taken : taken + FILL[q]]:
+                first_half(bt, chunk)
+            taken += FILL[q]
+            if q < ROUNDS - 1:
+                backs = [transpose_back(seconds, i) for i in range(TILES_MOVING)]
                 for i in range(TILES_MOVING):
-                    backs[(q, i)] = transpose_back(seconds, i)
+                    fold(TILES_MOVING * q + i, TILES_MOVING * h + i, jc, backs[i])
+                    if USUAL[i] != "S":
+                        store_unit(TILES_MOVING * q + i, TILES_MOVING * h + i, jc, USUAL[i])
             if q < 2:
                 for bt in (TILES_MOVING + 2 * q, TILES_MOVING + 2 * q + 1):
                     transpose_x(bt)
                     quantise_x(bt)
+        number = TILES_MOVING * (ROUNDS - 1)
+        for part in (0, 1):
+            halves = [transpose_back(seconds, i, (2 * part, 2 * part + 1), part == 1) for i in range(TILES_MOVING)]
+            for i in range(TILES_MOVING):
+                fold(number, TILES_MOVING + i, CHUNKS - 1, halves[i], 2 * P * part, 2 * P)
+                store_unit(number, TILES_MOVING + i, CHUNKS - 1, LAST[4 * part + i], 2 * P * part, 2 * P)
+                number += 1

@@ -289,7 +289,13 @@ def tile_middlelayer_kernel(tc, in_data, W_words, W_scales, bias, out):
                 first_half(bt, chunk)
             taken += FILL[q]
             if q < ROUNDS - 1:
-                backs = [transpose_back(seconds, i) for i in range(TILES_MOVING)]
+                backs = [back_pool.tile([P, CHUNK], F32, tag="back", name="back%d" % i) for i in range(TILES_MOVING)]
+                for sweep in (0, 1):
+                    for i in range(TILES_MOVING):
+                        for jt in (2 * sweep, 2 * sweep + 1):
+                            nc.tensor.transpose(
+                                backs[i][:, P * jt : P * (jt + 1)], seconds[jt][:, P * i : P * (i + 1)], identity[:]
+                            )
                 for i in range(TILES_MOVING):
                     fold(TILES_MOVING * q + i, TILES_MOVING * h + i, jc, backs[i])
                     if USUAL[i] != "S":

@@ -251,14 +251,14 @@ def tile_middlelayer_kernel(tc, in_data, W_words, W_scales, bias, out):
         quantise_x(0)
         transpose_x(1)
         copy_spread(1)
+        spread_bias(2)
+        spread_bias(3)
         quantise_x(1)
         sort_x(2)
         first_half(0, 0)
         sort_x(3)
         first_half(0, 1)
-        spread_bias(2)
         copy_spread(2)
-        spread_bias(3)
         copy_spread(3)
         first_half(1, 0)
         first_half(1, 1)
@@ -281,6 +281,10 @@ def tile_middlelayer_kernel(tc, in_data, W_words, W_scales, bias, out):
         for q in range(ROUNDS):
             h, jc = q // CHUNKS, q % CHUNKS
             seconds = [second_half(h, jc, jt) for jt in range(TILES_MOVING)]
+            if q in (1, 2):
+                for bt in (TILES_MOVING + 2 * (q - 1), TILES_MOVING + 2 * (q - 1) + 1):
+                    transpose_x(bt)
+                    quantise_x(bt)
             if q > 0:
                 for i in range(TILES_MOVING):
                     if USUAL[i] == "S":
@@ -300,10 +304,6 @@ def tile_middlelayer_kernel(tc, in_data, W_words, W_scales, bias, out):
                     fold(TILES_MOVING * q + i, TILES_MOVING * h + i, jc, backs[i])
                     if USUAL[i] != "S":
                         store_unit(TILES_MOVING * q + i, TILES_MOVING * h + i, jc, USUAL[i])
-            if q < 2:
-                for bt in (TILES_MOVING + 2 * q, TILES_MOVING + 2 * q + 1):
-                    transpose_x(bt)
-                    quantise_x(bt)
         number = TILES_MOVING * (ROUNDS - 1)
         for part in (0, 1):
             halves = [transpose_back(seconds, i, (2 * part, 2 * part + 1), part == 1) for i in range(TILES_MOVING)]

@@ -31,6 +31,7 @@ FLOPS = 2 * ROWS * K * COLS
 USUAL = "GSSV"
 LAST = "SGSVSGSV"
 FILL = (3, 3, 3, 3, 3, 3, 3, 3)
+WARM = 4
 
 
 def tile_middlelayer_kernel(tc, in_data, W_words, W_scales, bias, out):
@@ -59,16 +60,18 @@ def tile_middlelayer_kernel(tc, in_data, W_words, W_scales, bias, out):
         bias_rows = const.tile([P, P], BF16)
         bias_column = const.tile([P, COLS // P], F32)
         ones = const.tile([P, P], BF16)
+        warm_rhs = const.tile([P, CHUNK], BF16)
         identity = const.tile([P, P], F32)
         identity_bf16 = const.tile([P, P], BF16)
         folded = [const.tile([P, 2, CHUNK], F32, name="folded%d" % i) for i in range(ZERO_PLANE_TILES)]
 
+        nc.gpsimd.memset(ones[:], 1.0)
+        nc.vector.memset(warm_rhs[:].bitcast(I32), 0)
         nc.vector.memset(w_scales[:].bitcast(I32), 0)
         nc.gpsimd.memset(bias_rows[:].bitcast(F32), 0.0)
         nc.gpsimd.memset(bias_row[:].bitcast(F32), 0.0)
         make_identity(nc, identity[:])
         make_identity(nc, identity_bf16[:])
-        nc.gpsimd.memset(ones[:], 1.0)
 
         x_in = {}
 
@@ -87,7 +90,9 @@ def tile_middlelayer_kernel(tc, in_data, W_words, W_scales, bias, out):
             first_byte = 2 * (n0 % W_LOAD)
             return w_words[n0 // W_LOAD][:, g, first_byte : first_byte + 2 * width].bitcast(FP4X4)
 
-        load_x(0)
+        x_in[0] = xin_pool.tile([P, 2 * K], BF16, name="x_in")
+        for g in range(PASSES):
+            nc.sync.dma_start(out=x_in[0][:, K * g : K * (g + 1)], in_=in_data[0:P, K * g : K * (g + 1)])
         load_x(1)
         for r in range(4):
             nc.sync.dma_start(
@@ -127,14 +132,19 @@ def tile_middlelayer_kernel(tc, in_data, W_words, W_scales, bias, out):
 
         def transpose_x(bt):
             words = x_sorted[bt][:].bitcast(F32)
-            turned = sums_pool.tile([P, 2 * PASSES, P], F32, tag="sums")
-            for gu in range(2 * PASSES):
-                nc.tensor.transpose(turned[:, gu, :], words[:, P * gu : P * (gu + 1)], identity[:])
             x_grouped[bt] = grouped_pool.tile([P, PASSES * P * 4], BF16, name="x_grouped", align_bytes=64)
-            nc.scalar.copy(
-                out=x_grouped[bt][:].bitcast(F32).rearrange("p (g b u) -> p g b u", g=PASSES, b=P, u=2),
-                in_=turned[:].rearrange("p (g u) b -> p g b u", g=PASSES, u=2),
-            )
+            grouped = x_grouped[bt][:].bitcast(F32).rearrange("p (g b u) -> p g b u", g=PASSES, b=P, u=2)
+            if bt == 0:
+                for g in range(PASSES):
+                    turned = sums_pool.tile([P, 2, P], F32, tag="sums")
+                    for u in range(2):
+                        nc.tensor.transpose(turned[:, u, :], words[:, P * (2 * g + u) : P * (2 * g + u + 1)], identity[:])
+                    nc.scalar.copy(out=grouped[:, g], in_=turned[:].rearrange("p u b -> p b u"))
+            else:
+                turned = sums_pool.tile([P, 2 * PASSES, P], F32, tag="sums")
+                for gu in range(2 * PASSES):
+                    nc.tensor.transpose(turned[:, gu, :], words[:, P * gu : P * (gu + 1)], identity[:])
+                nc.scalar.copy(out=grouped, in_=turned[:].rearrange("p (g u) b -> p g b u", g=PASSES, u=2))
 
         def quantise_x(bt):
             rows = slice(P * bt, P * (bt + 1))
@@ -241,6 +251,9 @@ def tile_middlelayer_kernel(tc, in_data, W_words, W_scales, bias, out):
         def copy_spread(jc):
             nc.scalar.copy(out=bias_spread[:, CHUNK * jc : CHUNK * (jc + 1)], in_=spreads[jc][:])
 
+        warm = sums_pool.tile([P, CHUNK], F32, tag="sums")
+        for n in range(WARM):
+            nc.tensor.matmul(out=warm[:], lhsT=ones[:], rhs=warm_rhs[:], start=True, stop=True)
         sort_x(0)
         transpose_x(0)
         sort_x(1)

@@ -60,12 +60,14 @@ def tile_middlelayer_kernel(tc, in_data, W_words, W_scales, bias, out):
         bias_rows = const.tile([P, P], BF16)
         bias_column = const.tile([P, COLS // P], F32)
         ones = const.tile([P, P], BF16)
+        table_warmer = const.tile([P, 1], F32)
         warm_rhs = const.tile([P, CHUNK], BF16)
         identity = const.tile([P, P], F32)
         identity_bf16 = const.tile([P, P], BF16)
         folded = [const.tile([P, 2, CHUNK], F32, name="folded%d" % i) for i in range(ZERO_PLANE_TILES)]
 
         nc.gpsimd.memset(ones[:], 1.0)
+        nc.scalar.activation(out=table_warmer[:], in_=ones[:, 0:1], func=ACT.Relu)
         nc.vector.memset(warm_rhs[:].bitcast(I32), 0)
         nc.vector.memset(w_scales[:].bitcast(I32), 0)
         nc.gpsimd.memset(bias_rows[:].bitcast(F32), 0.0)

@@ -28,9 +28,10 @@ ZERO_PLANE_TILES = 6
 
 W_LOAD = 2 * CHUNK
 FLOPS = 2 * ROWS * K * COLS
-USUAL = "GSSV"
-LAST = "SGSVSGSV"
-FILL = (3, 3, 3, 3, 3, 3, 3, 3)
+USUAL = "GGSG"
+LAST = "SGSGSGSV"
+FILLS = (3, 3, 3, 3, 3, 3, 2)
+BEFORE_LAST = "GGGG"
 WARM = 4
 
 
@@ -292,37 +293,61 @@ def tile_middlelayer_kernel(tc, in_data, W_words, W_scales, bias, out):
 
         fillers = [(bt, jc) for jc in range(CHUNKS) for bt in (2, 3)]
         fillers += [(bt, jc) for jc in range(CHUNKS) for bt in range(TILES_MOVING, ROW_TILES)]
-        taken = 0
-        for q in range(ROUNDS):
+
+        def fill(count):
+            for n in range(min(count, len(fillers))):
+                first_half(*fillers.pop(0))
+
+        later = []
+
+        def scalars_next(count=1):
+            for n in range(min(count, len(later))):
+                store_unit(*later.pop(0))
+
+        for q in range(ROUNDS - 1):
             h, jc = q // CHUNKS, q % CHUNKS
-            seconds = [second_half(h, jc, jt) for jt in range(TILES_MOVING)]
+            usual = USUAL if q < ROUNDS - 2 else BEFORE_LAST
+            seconds = []
+            for jt in range(TILES_MOVING):
+                seconds.append(second_half(h, jc, jt))
             if q in (1, 2):
                 for bt in (TILES_MOVING + 2 * (q - 1), TILES_MOVING + 2 * (q - 1) + 1):
                     transpose_x(bt)
                     quantise_x(bt)
-            if q > 0:
+            scalars_next(TILES_MOVING)
+            fill(FILLS[q])
+            backs = [back_pool.tile([P, CHUNK], F32, tag="back", name="back%d" % i) for i in range(TILES_MOVING)]
+            for sweep in (0, 1):
                 for i in range(TILES_MOVING):
-                    if USUAL[i] == "S":
-                        store_unit(TILES_MOVING * (q - 1) + i, TILES_MOVING * ((q - 1) // CHUNKS) + i, (q - 1) % CHUNKS, "S")
-            for bt, chunk in fillers[taken : taken + FILL[q]]:
-                first_half(bt, chunk)
-            taken += FILL[q]
-            if q < ROUNDS - 1:
-                backs = [back_pool.tile([P, CHUNK], F32, tag="back", name="back%d" % i) for i in range(TILES_MOVING)]
-                for sweep in (0, 1):
-                    for i in range(TILES_MOVING):
-                        for jt in (2 * sweep, 2 * sweep + 1):
-                            nc.tensor.transpose(
-                                backs[i][:, P * jt : P * (jt + 1)], seconds[jt][:, P * i : P * (i + 1)], identity[:]
-                            )
-                for i in range(TILES_MOVING):
-                    fold(TILES_MOVING * q + i, TILES_MOVING * h + i, jc, backs[i])
-                    if USUAL[i] != "S":
-                        store_unit(TILES_MOVING * q + i, TILES_MOVING * h + i, jc, USUAL[i])
-        number = TILES_MOVING * (ROUNDS - 1)
-        for part in (0, 1):
-            halves = [transpose_back(seconds, i, (2 * part, 2 * part + 1), part == 1) for i in range(TILES_MOVING)]
+                    for jt in (2 * sweep, 2 * sweep + 1):
+                        nc.tensor.transpose(
+                            backs[i][:, P * jt : P * (jt + 1)], seconds[jt][:, P * i : P * (i + 1)], identity[:]
+                        )
             for i in range(TILES_MOVING):
-                fold(number, TILES_MOVING + i, CHUNKS - 1, halves[i], 2 * P * part, 2 * P)
-                store_unit(number, TILES_MOVING + i, CHUNKS - 1, LAST[4 * part + i], 2 * P * part, 2 * P)
-                number += 1
+                number, bt = TILES_MOVING * q + i, TILES_MOVING * h + i
+                fold(number, bt, jc, backs[i])
+                if usual[i] == "S":
+                    later.append((number, bt, jc, "S"))
+                else:
+                    store_unit(number, bt, jc, usual[i])
+
+        def finish(i, part, back):
+            number = TILES_MOVING * (ROUNDS - 1 + part) + i
+            fold(number, TILES_MOVING + i, CHUNKS - 1, back, 2 * P * part, 2 * P)
+            store_unit(number, TILES_MOVING + i, CHUNKS - 1, LAST[TILES_MOVING * part + i], 2 * P * part, 2 * P)
+
+        seconds = [second_half(1, CHUNKS - 1, 0)]
+        scalars_next()
+        seconds.append(second_half(1, CHUNKS - 1, 1))
+        scalars_next(TILES_MOVING)
+        fill(2)
+        halves = [transpose_back(seconds, i, (0, 1)) for i in range(TILES_MOVING)]
+        seconds += [second_half(1, CHUNKS - 1, jt) for jt in (2, 3)]
+        finish(0, 0, halves[0])
+        finish(1, 0, halves[1])
+        fill(2)
+        finish(2, 0, halves[2])
+        finish(3, 0, halves[3])
+        halves = [transpose_back(seconds, i, (2, 3), i >= 2) for i in range(TILES_MOVING)]
+        for i in range(TILES_MOVING):
+            finish(i, 1, halves[i])

@@ -33,6 +33,7 @@ LAST = "SGSGSGSV"
 FILLS = (3, 3, 3, 3, 3, 3, 2)
 BEFORE_LAST = "GGGG"
 WARM = 4
+ZERO_PLANES_BY_VECTOR = 3
 
 
 def tile_middlelayer_kernel(tc, in_data, W_words, W_scales, bias, out):
@@ -75,6 +76,12 @@ def tile_middlelayer_kernel(tc, in_data, W_words, W_scales, bias, out):
         nc.gpsimd.memset(bias_row[:].bitcast(F32), 0.0)
         make_identity(nc, identity[:])
         make_identity(nc, identity_bf16[:])
+
+        for n, tile in enumerate(folded):
+            if n < ZERO_PLANES_BY_VECTOR:
+                nc.vector.memset(tile[:, 1, :], 0.0)
+            else:
+                nc.gpsimd.memset(tile[:, 1, :], 0.0)
 
         x_in = {}
 
@@ -286,8 +293,6 @@ def tile_middlelayer_kernel(tc, in_data, W_words, W_scales, bias, out):
         first_half(0, 3, True)
         first_half(1, 2, True)
         first_half(1, 3, True)
-        for tile in folded:
-            nc.gpsimd.memset(tile[:, 1, :], 0.0)
         for bt in range(TILES_MOVING, ROW_TILES):
             sort_x(bt)
 

@@ -24,7 +24,7 @@ CHUNK = 512
 CHUNKS = HALF // CHUNK
 TILES_MOVING = CHUNK // P
 ROUNDS = (ROW_TILES // TILES_MOVING) * CHUNKS
-ZERO_PLANE_TILES = 6
+ZERO_PLANE_TILES = 4
 
 W_LOAD = 2 * CHUNK
 FLOPS = 2 * ROWS * K * COLS
@@ -57,9 +57,10 @@ def tile_middlelayer_kernel(tc, in_data, W_words, W_scales, bias, out):
         ]
         x_words = const.tile([P, PASSES, ROWS], U32, align_bytes=64)
         x_scales = const.tile([P, PASSES, ROWS], U8, align_bytes=64)
-        bias_row = const.tile([P, HALF], BF16)
+        bias_tile = const.tile([P, CHUNK + P], BF16)
+        bias_chunks = bias_tile[:, 0:CHUNK]
+        bias_rows = bias_tile[:, CHUNK : CHUNK + P]
         bias_spread = const.tile([P, HALF], BF16)
-        bias_rows = const.tile([P, P], BF16)
         bias_column = const.tile([P, COLS // P], F32)
         ones = const.tile([P, P], BF16)
         table_warmer = const.tile([P, 1], F32)
@@ -68,12 +69,13 @@ def tile_middlelayer_kernel(tc, in_data, W_words, W_scales, bias, out):
         identity_bf16 = const.tile([P, P], BF16)
         folded = [const.tile([P, 2, CHUNK], F32, name="folded%d" % i) for i in range(ZERO_PLANE_TILES)]
 
+        nc.gpsimd.memset(bias_tile[:].bitcast(F32), 0.0)
         nc.gpsimd.memset(ones[:], 1.0)
+        nc.scalar.dma_start(out=bias_tile[0:CHUNKS, 0:CHUNK], in_=bias[0:HALF].rearrange("(c n) -> c n", n=CHUNK))
+        nc.scalar.dma_start(out=bias_tile[0 : COLS // P, CHUNK : CHUNK + P], in_=bias.rearrange("(c p) -> c p", p=P))
         nc.scalar.activation(out=table_warmer[:], in_=ones[:, 0:1], func=ACT.Relu)
         nc.vector.memset(warm_rhs[:].bitcast(I32), 0)
         nc.vector.memset(w_scales[:].bitcast(I32), 0)
-        nc.gpsimd.memset(bias_rows[:].bitcast(F32), 0.0)
-        nc.gpsimd.memset(bias_row[:].bitcast(F32), 0.0)
         make_identity(nc, identity[:])
         make_identity(nc, identity_bf16[:])
 
@@ -100,28 +102,29 @@ def tile_middlelayer_kernel(tc, in_data, W_words, W_scales, bias, out):
             first_byte = 2 * (n0 % W_LOAD)
             return w_words[n0 // W_LOAD][:, g, first_byte : first_byte + 2 * width].bitcast(FP4X4)
 
+        def load_w_scales(n0, n1):
+            for r in range(4):
+                nc.sync.dma_start(
+                    out=w_scales[r : P : 32, :, n0:n1].bitcast(I32),
+                    in_=W_scales[:, r : 16 : 4, n0:n1].rearrange("g q n -> q g n").bitcast(I32),
+                )
+
         x_in[0] = xin_pool.tile([P, 2 * K], BF16, name="x_in")
         for g in range(PASSES):
             nc.sync.dma_start(out=x_in[0][:, K * g : K * (g + 1)], in_=in_data[0:P, K * g : K * (g + 1)])
         load_x(1)
-        for r in range(4):
-            nc.sync.dma_start(
-                out=w_scales[r : P : 32, :, :].bitcast(I32),
-                in_=W_scales[:, r : 16 : 4, :].rearrange("g q n -> q g n").bitcast(I32),
-            )
-        nc.scalar.dma_start(out=bias_row[0:1, :], in_=bias[0:HALF].rearrange("(o n) -> o n", o=1))
-        nc.scalar.dma_start(out=bias_rows[0 : COLS // P, :], in_=bias.rearrange("(c p) -> c p", p=P))
+        load_w_scales(0, HALF)
         load_w_words(0, 0)
         load_x(2)
         load_x(3)
         load_w_words(0, 1)
+        load_w_scales(HALF, COLS)
         load_w_words(1, 0)
         load_x(4)
         load_x(5)
         load_w_words(1, 1)
         load_x(6)
         load_x(7)
-
 
         x_sorted = {}
         x_grouped = {}
@@ -171,15 +174,15 @@ def tile_middlelayer_kernel(tc, in_data, W_words, W_scales, bias, out):
             spreads[jc] = back_pool.tile([P, CHUNK], F32, name="spread", tag="back")
             nc.tensor.matmul(
                 out=spreads[jc][:],
-                lhsT=ones[:],
-                rhs=bias_row[:, CHUNK * jc : CHUNK * (jc + 1)],
+                lhsT=identity_bf16[:, jc : jc + 1].to_broadcast([P, P]),
+                rhs=bias_chunks,
                 start=True,
                 stop=True,
             )
 
         def bias_onto_partitions():
             turned = sums_pool.tile([P, P], F32, tag="sums")
-            nc.tensor.matmul(out=turned[:], lhsT=bias_rows[:], rhs=identity_bf16[:], start=True, stop=True)
+            nc.tensor.matmul(out=turned[:], lhsT=bias_rows, rhs=identity_bf16[:], start=True, stop=True)
             nc.vector.tensor_copy(out=bias_column[:], in_=turned[:, 0 : COLS // P])
 
         first = {}

@@ -51,7 +51,7 @@ def tile_middlelayer_kernel(tc, in_data, W_words, W_scales, bias, out):
         back_pool = ctx.enter_context(tc.psum_pool(name="back", bufs=TILES_MOVING))
         ctx.enter_context(tc.manual_schedule())
 
-        w_scales = const.tile([P, PASSES, COLS], U8, align_bytes=64)
+        w_scales = [const.tile([P, PASSES, HALF], U8, align_bytes=64, name="w_scales%d" % half) for half in (0, 1)]
         w_words = [
             const.tile([P, PASSES, 2 * W_LOAD], U8, align_bytes=64, name="w_words%d" % i) for i in range(COLS // W_LOAD)
         ]
@@ -75,7 +75,8 @@ def tile_middlelayer_kernel(tc, in_data, W_words, W_scales, bias, out):
         nc.scalar.dma_start(out=bias_tile[0 : COLS // P, CHUNK : CHUNK + P], in_=bias.rearrange("(c p) -> c p", p=P))
         nc.scalar.activation(out=table_warmer[:], in_=ones[:, 0:1], func=ACT.Relu)
         nc.vector.memset(warm_rhs[:].bitcast(I32), 0)
-        nc.vector.memset(w_scales[:].bitcast(I32), 0)
+        for half in (0, 1):
+            nc.vector.memset(w_scales[half][:].bitcast(I32), 0)
         make_identity(nc, identity[:])
         make_identity(nc, identity_bf16[:])
 
@@ -102,23 +103,26 @@ def tile_middlelayer_kernel(tc, in_data, W_words, W_scales, bias, out):
             first_byte = 2 * (n0 % W_LOAD)
             return w_words[n0 // W_LOAD][:, g, first_byte : first_byte + 2 * width].bitcast(FP4X4)
 
-        def load_w_scales(n0, n1):
+        def load_w_scales(half):
             for r in range(4):
                 nc.sync.dma_start(
-                    out=w_scales[r : P : 32, :, n0:n1].bitcast(I32),
-                    in_=W_scales[:, r : 16 : 4, n0:n1].rearrange("g q n -> q g n").bitcast(I32),
+                    out=w_scales[half][r : P : 32, :, :].bitcast(I32),
+                    in_=W_scales[:, r : 16 : 4, HALF * half : HALF * (half + 1)].rearrange("g q n -> q g n").bitcast(I32),
                 )
+
+        def scale_columns(g, n0, width):
+            return w_scales[n0 // HALF][:, g, n0 % HALF : n0 % HALF + width]
 
         x_in[0] = xin_pool.tile([P, 2 * K], BF16, name="x_in")
         for g in range(PASSES):
             nc.sync.dma_start(out=x_in[0][:, K * g : K * (g + 1)], in_=in_data[0:P, K * g : K * (g + 1)])
         load_x(1)
-        load_w_scales(0, HALF)
+        load_w_scales(0)
         load_w_words(0, 0)
         load_x(2)
         load_x(3)
         load_w_words(0, 1)
-        load_w_scales(HALF, COLS)
+        load_w_scales(1)
         load_w_words(1, 0)
         load_x(4)
         load_x(5)
@@ -200,7 +204,7 @@ def tile_middlelayer_kernel(tc, in_data, W_words, W_scales, bias, out):
                     lhsT=x_words[:, g, rows].bitcast(FP8X4),
                     lhsT_scale=x_scales[:, g, rows],
                     rhs=w_columns(g, n0, CHUNK),
-                    rhs_scale=w_scales[:, g, n0 : n0 + CHUNK],
+                    rhs_scale=scale_columns(g, n0, CHUNK),
                     start=(g == 0),
                     stop=(g == PASSES - 1),
                 )
@@ -217,7 +221,7 @@ def tile_middlelayer_kernel(tc, in_data, W_words, W_scales, bias, out):
                 nc.tensor.matmul_mx(
                     out=sums[:],
                     lhsT=w_columns(g, n0, P),
-                    lhsT_scale=w_scales[:, g, n0 : n0 + P],
+                    lhsT_scale=scale_columns(g, n0, P),
                     rhs=x_words[:, g, rows].bitcast(FP8X4),
                     rhs_scale=x_scales[:, g, rows],
                     start=(g == 0),
@@ -318,12 +322,12 @@ def tile_middlelayer_kernel(tc, in_data, W_words, W_scales, bias, out):
             seconds = []
             for jt in range(TILES_MOVING):
                 seconds.append(second_half(h, jc, jt))
+            scalars_next(TILES_MOVING)
+            fill(FILLS[q])
             if q in (1, 2):
                 for bt in (TILES_MOVING + 2 * (q - 1), TILES_MOVING + 2 * (q - 1) + 1):
                     transpose_x(bt)
                     quantise_x(bt)
-            scalars_next(TILES_MOVING)
-            fill(FILLS[q])
             backs = [back_pool.tile([P, CHUNK], F32, tag="back", name="back%d" % i) for i in range(TILES_MOVING)]
             for sweep in (0, 1):
                 for i in range(TILES_MOVING):

from contextlib import ExitStack

import concourse.mybir as mybir
from concourse.masks import make_identity

F32 = mybir.dt.float32
BF16 = mybir.dt.bfloat16
I32 = mybir.dt.int32
U32 = mybir.dt.uint32
U8 = mybir.dt.uint8
FP8X4 = mybir.dt.float8_e4m3fn_x4
FP4X4 = mybir.dt.float4_e2m1fn_x4
ALU = mybir.AluOpType
ACT = mybir.ActivationFunctionType

P = 128
ROWS = 1024
K = 1024
COLS = 4096
HALF = COLS // 2
PASSES = K // 512
ROW_TILES = ROWS // P
CHUNK = 512
CHUNKS = HALF // CHUNK
TILES_MOVING = CHUNK // P
ROUNDS = (ROW_TILES // TILES_MOVING) * CHUNKS
ZERO_PLANE_TILES = 4

W_LOAD = 2 * CHUNK
FLOPS = 2 * ROWS * K * COLS
USUAL = "GGSG"
LAST = "SGSGSGSV"
FILLS = (3, 3, 3, 3, 3, 3, 2)
BEFORE_LAST = "GGGG"
WARM = 4
ZERO_PLANES_BY_VECTOR = 3


def tile_middlelayer_kernel(tc, in_data, W_words, W_scales, bias, out):
    nc = tc.nc
    out_rows = out.rearrange("b n o -> b (n o)")
    with ExitStack() as ctx:
        const = ctx.enter_context(tc.tile_pool(name="const", bufs=1))
        xin_pool = ctx.enter_context(tc.tile_pool(name="xin", bufs=ROW_TILES))
        sorted_pool = ctx.enter_context(tc.tile_pool(name="sorted", bufs=TILES_MOVING))
        grouped_pool = ctx.enter_context(tc.tile_pool(name="grouped", bufs=TILES_MOVING))
        first_pool = ctx.enter_context(tc.tile_pool(name="first", bufs=16))
        second_pool = ctx.enter_context(tc.tile_pool(name="second", bufs=2 * TILES_MOVING))
        store_pool = ctx.enter_context(tc.tile_pool(name="store", bufs=12))
        sums_pool = ctx.enter_context(tc.psum_pool(name="sums", bufs=4))
        back_pool = ctx.enter_context(tc.psum_pool(name="back", bufs=TILES_MOVING))
        ctx.enter_context(tc.manual_schedule())

        w_scales = [const.tile([P, PASSES, HALF], U8, align_bytes=64, name="w_scales%d" % half) for half in (0, 1)]
        w_words = [
            const.tile([P, PASSES, 2 * W_LOAD], U8, align_bytes=64, name="w_words%d" % i) for i in range(COLS // W_LOAD)
        ]
        x_words = const.tile([P, PASSES, ROWS], U32, align_bytes=64)
        x_scales = const.tile([P, PASSES, ROWS], U8, align_bytes=64)
        bias_tile = const.tile([P, CHUNK + P], BF16)
        bias_chunks = bias_tile[:, 0:CHUNK]
        bias_rows = bias_tile[:, CHUNK : CHUNK + P]
        bias_spread = const.tile([P, HALF], BF16)
        bias_column = const.tile([P, COLS // P], F32)
        ones = const.tile([P, P], BF16)
        table_warmer = const.tile([P, 1], F32)
        warm_rhs = const.tile([P, CHUNK], BF16)
        identity = const.tile([P, P], F32)
        identity_bf16 = const.tile([P, P], BF16)
        folded = [const.tile([P, 2, CHUNK], F32, name="folded%d" % i) for i in range(ZERO_PLANE_TILES)]

        nc.gpsimd.memset(bias_tile[:].bitcast(F32), 0.0)
        nc.gpsimd.memset(ones[:], 1.0)
        nc.scalar.dma_start(out=bias_tile[0:CHUNKS, 0:CHUNK], in_=bias[0:HALF].rearrange("(c n) -> c n", n=CHUNK))
        nc.scalar.dma_start(out=bias_tile[0 : COLS // P, CHUNK : CHUNK + P], in_=bias.rearrange("(c p) -> c p", p=P))
        nc.scalar.activation(out=table_warmer[:], in_=ones[:, 0:1], func=ACT.Relu)
        nc.vector.memset(warm_rhs[:].bitcast(I32), 0)
        for half in (0, 1):
            nc.vector.memset(w_scales[half][:].bitcast(I32), 0)
        make_identity(nc, identity[:])
        make_identity(nc, identity_bf16[:])

        for n, tile in enumerate(folded):
            if n < ZERO_PLANES_BY_VECTOR:
                nc.vector.memset(tile[:, 1, :], 0.0)
            else:
                nc.gpsimd.memset(tile[:, 1, :], 0.0)

        x_in = {}

        def load_x(bt):
            x_in[bt] = xin_pool.tile([P, 2 * K], BF16, name="x_in")
            nc.sync.dma_start(out=x_in[bt][:], in_=in_data[P * bt : P * (bt + 1), :])

        def load_w_words(half, pair):
            i = (HALF // W_LOAD) * half + pair
            nc.sync.dma_start(
                out=w_words[i][:].bitcast(I32),
                in_=W_words[:, :, 2 * W_LOAD * i : 2 * W_LOAD * (i + 1)].rearrange("g p n -> p g n").bitcast(I32),
            )

        def w_columns(g, n0, width):
            first_byte = 2 * (n0 % W_LOAD)
            return w_words[n0 // W_LOAD][:, g, first_byte : first_byte + 2 * width].bitcast(FP4X4)

        def load_w_scales(half):
            for r in range(4):
                nc.sync.dma_start(
                    out=w_scales[half][r : P : 32, :, :].bitcast(I32),
                    in_=W_scales[:, r : 16 : 4, HALF * half : HALF * (half + 1)].rearrange("g q n -> q g n").bitcast(I32),
                )

        def scale_columns(g, n0, width):
            return w_scales[n0 // HALF][:, g, n0 % HALF : n0 % HALF + width]

        x_in[0] = xin_pool.tile([P, 2 * K], BF16, name="x_in")
        for g in range(PASSES):
            nc.sync.dma_start(out=x_in[0][:, K * g : K * (g + 1)], in_=in_data[0:P, K * g : K * (g + 1)])
        load_x(1)
        load_w_scales(0)
        load_w_words(0, 0)
        load_x(2)
        load_x(3)
        load_w_words(0, 1)
        load_w_scales(1)
        load_w_words(1, 0)
        load_x(4)
        load_x(5)
        load_w_words(1, 1)
        load_x(6)
        load_x(7)

        x_sorted = {}
        x_grouped = {}

        def sort_x(bt):
            x_sorted[bt] = sorted_pool.tile([P, K], BF16, name="x_sorted")
            imag = x_in[bt][:, 1 : 2 * K : 2].rearrange("b (g p u e) -> b g u p e", g=PASSES, p=P, u=2, e=2)
            dst = x_sorted[bt][:].rearrange("b (g u p e) -> b g u p e", g=PASSES, u=2, p=P, e=2)
            for g in range(PASSES):
                if bt in (0, 1) or (bt in (2, 3) and g == 0):
                    nc.vector.tensor_copy(out=dst[:, g], in_=imag[:, g])
                elif bt in (2, 3):
                    nc.scalar.copy(out=dst[:, g], in_=imag[:, g])
                else:
                    nc.gpsimd.tensor_scalar(
                        out=dst[:, g], in0=imag[:, g], scalar1=1.0, scalar2=0.0, op0=ALU.mult, op1=ALU.add
                    )

        def transpose_x(bt):
            words = x_sorted[bt][:].bitcast(F32)
            x_grouped[bt] = grouped_pool.tile([P, PASSES * P * 4], BF16, name="x_grouped", align_bytes=64)
            grouped = x_grouped[bt][:].bitcast(F32).rearrange("p (g b u) -> p g b u", g=PASSES, b=P, u=2)
            if bt == 0:
                for g in range(PASSES):
                    turned = sums_pool.tile([P, 2, P], F32, tag="sums")
                    for u in range(2):
                        nc.tensor.transpose(turned[:, u, :], words[:, P * (2 * g + u) : P * (2 * g + u + 1)], identity[:])
                    nc.scalar.copy(out=grouped[:, g], in_=turned[:].rearrange("p u b -> p b u"))
            else:
                turned = sums_pool.tile([P, 2 * PASSES, P], F32, tag="sums")
                for gu in range(2 * PASSES):
                    nc.tensor.transpose(turned[:, gu, :], words[:, P * gu : P * (gu + 1)], identity[:])
                nc.scalar.copy(out=grouped, in_=turned[:].rearrange("p (g u) b -> p g b u", g=PASSES, u=2))

        def quantise_x(bt):
            rows = slice(P * bt, P * (bt + 1))
            for g in range(PASSES):
                nc.vector.quantize_mx(
                    out=x_words[:, g, rows].bitcast(FP8X4),
                    scales=x_scales[:, g, rows],
                    in_=x_grouped[bt][:, 4 * P * g : 4 * P * (g + 1)],
                )

        spreads = {}

        def spread_bias(jc):
            spreads[jc] = back_pool.tile([P, CHUNK], F32, name="spread", tag="back")
            nc.tensor.matmul(
                out=spreads[jc][:],
                lhsT=identity_bf16[:, jc : jc + 1].to_broadcast([P, P]),
                rhs=bias_chunks,
                start=True,
                stop=True,
            )

        def bias_onto_partitions():
            turned = sums_pool.tile([P, P], F32, tag="sums")
            nc.tensor.matmul(out=turned[:], lhsT=bias_rows, rhs=identity_bf16[:], start=True, stop=True)
            nc.vector.tensor_copy(out=bias_column[:], in_=turned[:, 0 : COLS // P])

        first = {}

        def first_half(bt, jc, spare_bank=False):
            rows = slice(P * bt, P * (bt + 1))
            n0 = CHUNK * jc
            if spare_bank:
                sums = back_pool.tile([P, CHUNK], F32, tag="back")
            else:
                sums = sums_pool.tile([P, CHUNK], F32, tag="sums")
            for g in range(PASSES):
                nc.tensor.matmul_mx(
                    out=sums[:],
                    lhsT=x_words[:, g, rows].bitcast(FP8X4),
                    lhsT_scale=x_scales[:, g, rows],
                    rhs=w_columns(g, n0, CHUNK),
                    rhs_scale=scale_columns(g, n0, CHUNK),
                    start=(g == 0),
                    stop=(g == PASSES - 1),
                )
            first[(bt, jc)] = first_pool.tile([P, CHUNK], F32, name="first")
            nc.vector.tensor_tensor(
                out=first[(bt, jc)][:], in0=sums[:], in1=bias_spread[:, n0 : n0 + CHUNK], op=ALU.add
            )

        def second_half(h, jc, jt):
            rows = slice(CHUNK * h, CHUNK * (h + 1))
            n0 = HALF + CHUNK * jc + P * jt
            sums = sums_pool.tile([P, CHUNK], F32, tag="sums")
            for g in range(PASSES):
                nc.tensor.matmul_mx(
                    out=sums[:],
                    lhsT=w_columns(g, n0, P),
                    lhsT_scale=scale_columns(g, n0, P),
                    rhs=x_words[:, g, rows].bitcast(FP8X4),
                    rhs_scale=x_scales[:, g, rows],
                    start=(g == 0),
                    stop=(g == PASSES - 1),
                )
            second = second_pool.tile([P, CHUNK], F32)
            nc.scalar.activation(
                out=second[:], in_=sums[:], func=ACT.Relu, bias=bias_column[:, n0 // P : n0 // P + 1], scale=1.0
            )
            return second

        def transpose_back(seconds, i, tiles=(0, 1, 2, 3), spare_bank=False):
            if spare_bank:
                back = sums_pool.tile([P, P * len(tiles)], F32, tag="sums")
            else:
                back = back_pool.tile([P, P * len(tiles)], F32, tag="back")
            for n, jt in enumerate(tiles):
                nc.tensor.transpose(back[:, P * n : P * (n + 1)], seconds[jt][:, P * i : P * (i + 1)], identity[:])
            return back

        def fold(number, bt, jc, back, j0=0, width=CHUNK):
            planes = folded[number % ZERO_PLANE_TILES]
            nc.vector.scalar_tensor_tensor(
                out=planes[:, 0, 0:width], in0=first[(bt, jc)][:, j0 : j0 + width], scalar=0.0, in1=back[:], op0=ALU.max, op1=ALU.subtract
            )

        def store_unit(number, bt, jc, engine, j0=0, width=CHUNK):
            planes = folded[number % ZERO_PLANE_TILES]
            store = store_pool.tile([P, 2 * width], F32, name="store")
            pairs = store[:].rearrange("p (j e) -> p j e", e=2)
            alternately = planes[:, :, 0:width].rearrange("p e j -> p j e")
            if engine == "G":
                nc.gpsimd.tensor_scalar(
                    out=pairs, in0=alternately, scalar1=1.0, scalar2=0.0, op0=ALU.mult, op1=ALU.add
                )
            elif engine == "S":
                nc.scalar.copy(out=pairs, in_=alternately)
            else:
                nc.vector.tensor_copy(out=pairs, in_=alternately)
            nc.sync.dma_start(
                out=out_rows[P * bt : P * (bt + 1), 2 * (CHUNK * jc + j0) : 2 * (CHUNK * jc + j0 + width)], in_=store[:]
            )

        def copy_spread(jc):
            nc.scalar.copy(out=bias_spread[:, CHUNK * jc : CHUNK * (jc + 1)], in_=spreads[jc][:])

        warm = sums_pool.tile([P, CHUNK], F32, tag="sums")
        for n in range(WARM):
            nc.tensor.matmul(out=warm[:], lhsT=ones[:], rhs=warm_rhs[:], start=True, stop=True)
        sort_x(0)
        transpose_x(0)
        sort_x(1)
        bias_onto_partitions()
        spread_bias(0)
        copy_spread(0)
        spread_bias(1)
        quantise_x(0)
        transpose_x(1)
        copy_spread(1)
        spread_bias(2)
        spread_bias(3)
        quantise_x(1)
        sort_x(2)
        first_half(0, 0)
        sort_x(3)
        first_half(0, 1)
        copy_spread(2)
        copy_spread(3)
        first_half(1, 0)
        first_half(1, 1)
        transpose_x(2)
        transpose_x(3)
        quantise_x(2)
        quantise_x(3)
        first_half(0, 2, True)
        first_half(0, 3, True)
        first_half(1, 2, True)
        first_half(1, 3, True)
        for bt in range(TILES_MOVING, ROW_TILES):
            sort_x(bt)

        fillers = [(bt, jc) for jc in range(CHUNKS) for bt in (2, 3)]
        fillers += [(bt, jc) for jc in range(CHUNKS) for bt in range(TILES_MOVING, ROW_TILES)]

        def fill(count):
            for n in range(min(count, len(fillers))):
                first_half(*fillers.pop(0))

        later = []

        def scalars_next(count=1):
            for n in range(min(count, len(later))):
                store_unit(*later.pop(0))

        for q in range(ROUNDS - 1):
            h, jc = q // CHUNKS, q % CHUNKS
            usual = USUAL if q < ROUNDS - 2 else BEFORE_LAST
            seconds = []
            for jt in range(TILES_MOVING):
                seconds.append(second_half(h, jc, jt))
            scalars_next(TILES_MOVING)
            fill(FILLS[q])
            if q in (1, 2):
                for bt in (TILES_MOVING + 2 * (q - 1), TILES_MOVING + 2 * (q - 1) + 1):
                    transpose_x(bt)
                    quantise_x(bt)
            backs = [back_pool.tile([P, CHUNK], F32, tag="back", name="back%d" % i) for i in range(TILES_MOVING)]
            for sweep in (0, 1):
                for i in range(TILES_MOVING):
                    for jt in (2 * sweep, 2 * sweep + 1):
                        nc.tensor.transpose(
                            backs[i][:, P * jt : P * (jt + 1)], seconds[jt][:, P * i : P * (i + 1)], identity[:]
                        )
            for i in range(TILES_MOVING):
                number, bt = TILES_MOVING * q + i, TILES_MOVING * h + i
                fold(number, bt, jc, backs[i])
                if usual[i] == "S":
                    later.append((number, bt, jc, "S"))
                else:
                    store_unit(number, bt, jc, usual[i])

        def finish(i, part, back):
            number = TILES_MOVING * (ROUNDS - 1 + part) + i
            fold(number, TILES_MOVING + i, CHUNKS - 1, back, 2 * P * part, 2 * P)
            store_unit(number, TILES_MOVING + i, CHUNKS - 1, LAST[TILES_MOVING * part + i], 2 * P * part, 2 * P)

        seconds = [second_half(1, CHUNKS - 1, 0)]
        scalars_next()
        seconds.append(second_half(1, CHUNKS - 1, 1))
        scalars_next(TILES_MOVING)
        fill(2)
        halves = [transpose_back(seconds, i, (0, 1)) for i in range(TILES_MOVING)]
        seconds += [second_half(1, CHUNKS - 1, jt) for jt in (2, 3)]
        finish(0, 0, halves[0])
        finish(1, 0, halves[1])
        fill(2)
        finish(2, 0, halves[2])
        finish(3, 0, halves[3])
        halves = [transpose_back(seconds, i, (2, 3), i >= 2) for i in range(TILES_MOVING)]
        for i in range(TILES_MOVING):
            finish(i, 1, halves[i])
